import numpy as np
import ml_dtypes


def mxq(x, axis, fmt="e4m3"):
    dtype, down = {"e4m3": (ml_dtypes.float8_e4m3fn, 7), "e5m2": (ml_dtypes.float8_e5m2, 14)}[fmt]
    v = np.moveaxis(np.asarray(x, np.float32).astype(ml_dtypes.bfloat16).astype(np.float64), axis, -1)
    blocks = v.reshape(v.shape[:-1] + (-1, 32))
    amax = np.abs(blocks).max(-1, keepdims=True)
    byte = np.maximum(np.where(amax > 0, np.frexp(amax)[1] - 1 + 127, 0) - down, 1)
    scale = np.exp2(byte - 127.0)
    codes = (blocks / scale).astype(np.float32).astype(dtype).astype(np.float64)
    return np.moveaxis((codes * scale).reshape(v.shape), -1, axis)


WIDE = False


def mx_kscale(k):
    if not WIDE:
        return np.ones(k)
    levels = np.array([10, -10, 5, -5, 0])
    a = np.random.permutation(np.resize(levels, k // 512 * 4)).reshape(k // 512, 4)
    idx = np.arange(k)
    return np.exp2(a[idx // 512, idx % 128 // 32])


BF16 = ml_dtypes.bfloat16


def bf(x):
    return np.asarray(x, np.float32).astype(BF16)


def f64(x):
    return np.asarray(x).astype(np.float64)


E2M1 = np.array([0.0, 0.5, 1.0, 1.5, 2.0, 3.0, 4.0, 6.0, -0.0, -0.5, -1.0, -1.5, -2.0, -3.0, -4.0, -6.0])


def pack_weight(w, fmt):
    k, n = w.shape
    w = f64(bf(w)).reshape(k // 32, 32, n)
    amax = np.abs(w).max(1)
    if fmt == "e4m3":
        byte = np.frexp(amax)[1] - 1 + 127 - 7
    else:
        mant, ex = np.frexp(amax / 6.0)
        byte = np.where(mant > 0.5, ex, ex - 1) + 127
    byte = np.clip(np.where(amax > 0, byte, 1), 1, 254)
    scaled = (w * np.exp2(127.0 - byte)[:, None, :]).reshape(k, n).astype(np.float32)
    by_word = np.ascontiguousarray(scaled.reshape(k // 512, 128, 4, n).transpose(0, 1, 3, 2))
    if fmt == "e4m3":
        words = by_word.astype(ml_dtypes.float8_e4m3fn).view(np.uint8)
    else:
        c = by_word.astype(ml_dtypes.float4_e2m1fn).view(np.uint8) & 0xF
        words = c[..., 0::2] | (c[..., 1::2] << 4)
    return np.ascontiguousarray(words), np.ascontiguousarray(byte.astype(np.uint8).reshape(k // 512, 16, n))


def unpack_weight(words, scales, fmt):
    g, p, n, _ = words.shape
    if fmt == "e4m3":
        vals = np.ascontiguousarray(words).view(ml_dtypes.float8_e4m3fn).astype(np.float64)
    else:
        nib = np.empty((g, p, n, 4), np.uint8)
        nib[..., 0::2] = words & 0xF
        nib[..., 1::2] = words >> 4
        vals = E2M1[nib]
    vals = vals * np.repeat(np.exp2(scales.astype(np.float64) - 127.0), 8, axis=1)[..., None]
    return vals.transpose(0, 1, 3, 2).reshape(g * 512, n)


B, S, D, H, QL, KL, ND, VD, RD = 4, 64, 512, 16, 8192, 512, 64, 128, 64
QH = ND + RD
BASE = 10000.0


def rope(v):
    d = v.shape[-1]
    inv_freq = BASE ** (-np.arange(0, d, 2) / d)
    ang = np.arange(v.shape[1])[:, None] * inv_freq[None, :]
    cos = np.cos(ang)[None, :, None, :]
    sin = np.sin(ang)[None, :, None, :]
    v1 = v[..., 0::2]
    v2 = v[..., 1::2]
    o1 = v1 * cos - v2 * sin
    o2 = v1 * sin + v2 * cos
    return np.stack([o1, o2], axis=-1).reshape(v.shape)


def setup_inputs():
    s, t = mx_kscale(D), mx_kscale(QL)
    x = bf(np.random.standard_normal((B, S, D)) * s)
    Wqa_words, Wqa_scales = pack_weight(np.random.standard_normal((D, QL)) / np.sqrt(D) / s[:, None] * t, "e4m3")
    Wqb_words, Wqb_scales = pack_weight(np.random.standard_normal((QL, H * QH)) / np.sqrt(QL) / t[:, None], "e4m3")
    return {"x": x,
            "Wqa_words": Wqa_words, "Wqa_scales": Wqa_scales,
            "Wqb_words": Wqb_words, "Wqb_scales": Wqb_scales}


def reference(x, Wqa_words, Wqa_scales, Wqb_words, Wqb_scales):
    cq = mxq(f64(x), 2, "e4m3") @ unpack_weight(Wqa_words, Wqa_scales, "e4m3")
    q = (mxq(cq, 2, "e4m3") @ unpack_weight(Wqb_words, Wqb_scales, "e4m3")).reshape(B, S, H, QH)
    q_nope, q_pe = q[..., :ND], q[..., ND:]
    return np.concatenate([q_nope, rope(q_pe)], axis=-1)

@@ -1,0 +1,289 @@
+import math
+from contextlib import ExitStack
+
+import concourse.mybir as mybir
+from concourse.masks import make_identity
+
+F32 = mybir.dt.float32
+BF16 = mybir.dt.bfloat16
+I32 = mybir.dt.int32
+U32 = mybir.dt.uint32
+U8 = mybir.dt.uint8
+FP8X4 = mybir.dt.float8_e4m3fn_x4
+ALU = mybir.AluOpType
+FUNC = mybir.ActivationFunctionType
+
+P = 128
+K_PASS = 512
+BANK = 512
+TOKEN_TILES = 2
+LATENT = 8192
+GROUPS = LATENT // K_PASS
+Q_OUT = 2048
+ROUND = 1024
+ROUND_BANKS = ROUND // BANK
+HEAD = 128
+PLAIN = 64
+PAIRS = 32
+HEADS_PER_BANK = BANK // HEAD
+POSITIONS = 64
+PLANES = 4
+LAG = 3
+SPLIT = 10
+
+ROPE_BASE = 10000.0
+ROUND_MAGIC = 12582912.0
+
+FLOPS = 2 * 256 * 512 * LATENT + 2 * 256 * LATENT * Q_OUT
+
+
+def tile_multilatentattention_pa_k_kernel(tc, x, Wqa_words, Wqa_scales, Wqb_words, Wqb_scales, out):
+    nc = tc.nc
+    x_rows = x.flatten_outer_dims().rearrange("(a r) d -> r a d", r=P)
+    out_rows = out.rearrange("b s h d -> (b s) (h d)")
+    wqa_dram = Wqa_words[0].rearrange("p n t -> p (n t)").bitcast(I32)
+
+    with ExitStack() as ctx:
+        keep = ctx.enter_context(tc.tile_pool(name="keep", bufs=1))
+        rows_pool = ctx.enter_context(tc.tile_pool(name="rows", bufs=4))
+        grouped_pool = ctx.enter_context(tc.tile_pool(name="grouped", bufs=3))
+        result_pool = ctx.enter_context(tc.tile_pool(name="result", bufs=4))
+        rope_pool = ctx.enter_context(tc.tile_pool(name="rope", bufs=2))
+        psum = ctx.enter_context(tc.psum_pool(name="psum", bufs=1))
+        ctx.enter_context(tc.manual_schedule())
+
+        x_sb = keep.tile([P, TOKEN_TILES, K_PASS], BF16)
+        identity = keep.tile([P, P], F32)
+        x_grouped = keep.tile([P, TOKEN_TILES, P, 4], BF16, align_bytes=64)
+        x_codes = keep.tile([P, TOKEN_TILES * P], U32, align_bytes=64)
+        x_scales = keep.tile([P, TOKEN_TILES * P], U8, align_bytes=64)
+        wqa_words = keep.tile([P, LATENT], U32, align_bytes=64)
+        wqa_planes = keep.tile([P, LATENT // PLANES], U8, align_bytes=64)
+        wqb_words = keep.tile([P, GROUPS, Q_OUT], U32, align_bytes=64)
+        wqb_planes = keep.tile([P, GROUPS // PLANES, Q_OUT], U8, align_bytes=64)
+        cq_codes = keep.tile([P, GROUPS, TOKEN_TILES * P], U32, align_bytes=64)
+        cq_scales = keep.tile([P, GROUPS, TOKEN_TILES * P], U8, align_bytes=64)
+
+        nc.vector.memset(wqa_planes[:].bitcast(I32), 0)
+        nc.vector.memset(wqb_planes[:].bitcast(I32), 0)
+
+        zero = keep.tile([P, 1], F32)
+        warm = keep.tile([P, 1], F32)
+        nc.vector.memset(zero[:], 0.0)
+        nc.scalar.activation(out=warm[:], in_=zero[:], func=FUNC.Sin)
+
+        make_identity(nc, identity[:])
+
+        inv_freq = keep.tile([P, PAIRS], F32)
+        position = keep.tile([P, PAIRS], F32)
+        angle = keep.tile([P, PAIRS], F32)
+        turns = keep.tile([P, 2, PAIRS], F32)
+        lifted = keep.tile([P, 2, PAIRS], F32)
+        whole = keep.tile([P, 2, PAIRS], F32)
+        frac = keep.tile([P, 2, PAIRS], F32)
+        nc.gpsimd.memset(inv_freq[:, 0:1], 1.0)
+        for width in (1, 2, 4, 8, 16):
+            nc.gpsimd.tensor_scalar(
+                out=inv_freq[:, width : 2 * width],
+                in0=inv_freq[:, 0:width],
+                scalar1=ROPE_BASE ** (-2.0 * width / (2 * PAIRS)),
+                scalar2=0.0,
+                op0=ALU.mult,
+                op1=ALU.add,
+            )
+        for half in range(P // POSITIONS):
+            nc.gpsimd.iota(
+                position[half * POSITIONS : (half + 1) * POSITIONS, :],
+                pattern=[[0, PAIRS]],
+                base=0,
+                channel_multiplier=1,
+                allow_small_or_imprecise_dtypes=True,
+            )
+        nc.gpsimd.tensor_tensor(out=angle[:], in0=position[:], in1=inv_freq[:], op=ALU.mult)
+        for shifted in range(2):
+            nc.gpsimd.tensor_scalar(
+                out=turns[:, shifted, :],
+                in0=angle[:],
+                scalar1=1.0 / (2.0 * math.pi),
+                scalar2=0.25 * shifted,
+                op0=ALU.mult,
+                op1=ALU.add,
+            )
+        nc.gpsimd.tensor_single_scalar(out=lifted[:], in_=turns[:], scalar=ROUND_MAGIC, op=ALU.add)
+        nc.gpsimd.tensor_single_scalar(out=whole[:], in_=lifted[:], scalar=ROUND_MAGIC, op=ALU.subtract)
+        nc.gpsimd.tensor_tensor(out=frac[:], in0=turns[:], in1=whole[:], op=ALU.subtract)
+
+        def load_wqa_planes():
+            for quadrant in range(4):
+                nc.sync.dma_start(
+                    out=wqa_planes[32 * quadrant : 32 * quadrant + 16, :].bitcast(I32),
+                    in_=Wqa_scales[0, 4 * quadrant : 4 * quadrant + 4, :]
+                    .rearrange("r (j n) -> j r n", j=PLANES)
+                    .bitcast(I32),
+                )
+
+        def load_wqb_planes(plane_set):
+            for quadrant in range(4):
+                nc.sync.dma_start(
+                    out=wqb_planes[32 * quadrant : 32 * quadrant + 16, plane_set, :].bitcast(I32),
+                    in_=Wqb_scales[
+                        PLANES * plane_set : PLANES * (plane_set + 1), 4 * quadrant : 4 * quadrant + 4, :
+                    ].bitcast(I32),
+                )
+
+        def load_wqa_words(first_group, groups):
+            cols = slice(first_group * K_PASS, (first_group + groups) * K_PASS)
+            nc.sync.dma_start(out=wqa_words[:, cols].bitcast(I32), in_=wqa_dram[:, cols])
+
+        def load_wqb_words(g, q_round):
+            cols = slice(q_round * ROUND, (q_round + 1) * ROUND)
+            nc.sync.dma_start(
+                out=wqb_words[:, g, cols].bitcast(I32),
+                in_=Wqb_words[g].rearrange("p n t -> p (n t)").bitcast(I32)[:, cols],
+            )
+
+        nc.sync.dma_start(out=x_sb[:], in_=x_rows)
+        load_wqa_planes()
+        for g in range(GROUPS + LAG):
+            if g < GROUPS and g % 2 == 0:
+                load_wqa_words(g, 2)
+            if g >= LAG:
+                if (g - LAG) % PLANES == 0:
+                    load_wqb_planes((g - LAG) // PLANES)
+                load_wqb_words(g - LAG, 0)
+        for g in range(GROUPS):
+            load_wqb_words(g, 1)
+
+        x_words = x_sb[:].bitcast(F32)
+        x_flipped = psum.tile([P, TOKEN_TILES, 2, P], F32, tag="work2")
+        for a in range(TOKEN_TILES):
+            for u in range(2):
+                nc.tensor.transpose(out=x_flipped[:, a, u, :], in_=x_words[:, a, u : K_PASS // 2 : 2], identity=identity[:])
+        nc.vector.tensor_copy(out=x_grouped[:].bitcast(F32), in_=x_flipped[:].rearrange("p a u r -> p a r u"))
+        nc.vector.quantize_mx(
+            out=x_codes[:].bitcast(FP8X4),
+            scales=x_scales[:],
+            in_=x_grouped[:].rearrange("p a r t -> p (a r t)"),
+        )
+
+        def token_cols(a):
+            return slice(a * P, (a + 1) * P)
+
+        cq_rows = {}
+
+        def first_product(g):
+            cq_rows[g] = rows_pool.tile([P, TOKEN_TILES, 2, 2 * P], BF16, name="cq_rows")
+            plane = g // PLANES
+            block = g % PLANES
+            for a in range(TOKEN_TILES):
+                bank = psum.tile([P, BANK], F32, tag="work%d" % a, name="cq_bank")
+                nc.tensor.matmul_mx(
+                    out=bank[:],
+                    lhsT=x_codes[:, token_cols(a)].bitcast(FP8X4),
+                    lhsT_scale=x_scales[:, token_cols(a)],
+                    rhs=wqa_words[:, g * K_PASS : (g + 1) * K_PASS].bitcast(FP8X4),
+                    rhs_scale=wqa_planes[4 * plane : P, block * K_PASS : (block + 1) * K_PASS],
+                    start=True,
+                    stop=True,
+                )
+                sorted_view = cq_rows[g][:, a, :, :].rearrange("r u (p e) -> r u p e", e=2)
+                bank_view = bank[:].rearrange("r (p u e) -> r u p e", u=2, e=2)
+                if a == 0:
+                    nc.scalar.copy(out=sorted_view, in_=bank_view)
+                else:
+                    nc.vector.tensor_copy(out=sorted_view, in_=bank_view)
+
+        def flip_and_quantise(g):
+            flipped = psum.tile([P, TOKEN_TILES, 2, P], F32, tag="work%d" % (2 + g % 2), name="flipped")
+            for a in range(TOKEN_TILES):
+                for u in range(2):
+                    nc.tensor.transpose(
+                        out=flipped[:, a, u, :], in_=cq_rows[g][:, a, u, :].bitcast(F32), identity=identity[:]
+                    )
+            grouped = grouped_pool.tile([P, TOKEN_TILES, P, 4], BF16, align_bytes=64, name="grouped")
+            nc.scalar.copy(out=grouped[:].bitcast(F32), in_=flipped[:].rearrange("p a u r -> p a r u"))
+            nc.vector.quantize_mx(
+                out=cq_codes[:, g, :].bitcast(FP8X4),
+                scales=cq_scales[:, g, :],
+                in_=grouped[:].rearrange("p a r t -> p (a r t)"),
+            )
+
+        def second_product(bank, g, a, col0):
+            nc.tensor.matmul_mx(
+                out=bank[:],
+                lhsT=cq_codes[:, g, token_cols(a)].bitcast(FP8X4),
+                lhsT_scale=cq_scales[:, g, token_cols(a)],
+                rhs=wqb_words[:, g, col0 : col0 + BANK].bitcast(FP8X4),
+                rhs_scale=wqb_planes[4 * (g % PLANES) : P, g // PLANES, col0 : col0 + BANK],
+                start=(g == 0),
+                stop=(g == GROUPS - 1),
+            )
+
+        sin_pairs = keep.tile([P, PAIRS, 2], F32)
+        cos_pairs = keep.tile([P, PAIRS, 2], F32)
+
+        def rotate_and_store(bank, a, col0):
+            result = result_pool.tile([P, HEADS_PER_BANK, HEAD], F32, name="result")
+            same = rope_pool.tile([P, HEADS_PER_BANK, 2 * PAIRS], F32, name="same")
+            cross = rope_pool.tile([P, HEADS_PER_BANK, 2 * PAIRS], F32, name="cross")
+            table_shape = [P, HEADS_PER_BANK, 2 * PAIRS]
+            nc.scalar.copy(out=result[:], in_=bank[:].rearrange("r (h d) -> r h d", d=HEAD))
+            nc.vector.tensor_tensor(
+                out=same[:],
+                in0=result[:, :, PLAIN:HEAD],
+                in1=cos_pairs[:].rearrange("p j e -> p (j e)").unsqueeze(1).to_broadcast(table_shape),
+                op=ALU.mult,
+            )
+            nc.vector.tensor_tensor(
+                out=cross[:],
+                in0=result[:, :, PLAIN:HEAD],
+                in1=sin_pairs[:].rearrange("p j e -> p (j e)").unsqueeze(1).to_broadcast(table_shape),
+                op=ALU.mult,
+            )
+            for e in range(2):
+                nc.vector.tensor_tensor(
+                    out=result[:, :, PLAIN + e : HEAD : 2],
+                    in0=same[:, :, e : 2 * PAIRS : 2],
+                    in1=cross[:, :, 1 - e : 2 * PAIRS : 2],
+                    op=ALU.add,
+                )
+            nc.sync.dma_start(
+                out=out_rows[a * P : (a + 1) * P, col0 : col0 + BANK], in_=result[:].rearrange("r h d -> r (h d)")
+            )
+
+        banks_of_round = [(a, n) for a in range(TOKEN_TILES) for n in range(ROUND_BANKS)]
+        first_banks = {}
+        for a, n in banks_of_round:
+            first_banks[(a, n)] = psum.tile([P, BANK], F32, tag="first%d" % (ROUND_BANKS * a + n), name="first_bank")
+
+        for g in range(GROUPS + LAG):
+            if g < GROUPS:
+                first_product(g)
+            if g >= LAG:
+                for a, n in banks_of_round:
+                    second_product(first_banks[(a, n)], g - LAG, a, n * BANK)
+            if g < GROUPS and g % 2 == 1:
+                flip_and_quantise(g - 1)
+                flip_and_quantise(g)
+
+        nc.scalar.activation(out=sin_pairs[:, :, 0], in_=frac[:, 0, :], func=FUNC.Sin, scale=2.0 * math.pi)
+        nc.scalar.activation(out=sin_pairs[:, :, 1], in_=frac[:, 0, :], func=FUNC.Sin, scale=-2.0 * math.pi)
+        nc.scalar.activation(
+            out=cos_pairs[:],
+            in_=frac[:, 1, :].unsqueeze(2).to_broadcast([P, PAIRS, 2]),
+            func=FUNC.Sin,
+            scale=2.0 * math.pi,
+        )
+        for a, n in banks_of_round:
+            rotate_and_store(first_banks[(a, n)], a, n * BANK)
+
+        second_banks = {}
+        for a, n in banks_of_round:
+            second_banks[(a, n)] = psum.tile([P, BANK], F32, tag="work%d" % (ROUND_BANKS * a + n), name="second_bank")
+        for g in range(SPLIT):
+            for a, n in banks_of_round:
+                second_product(second_banks[(a, n)], g, a, ROUND + n * BANK)
+        for a, n in banks_of_round:
+            for g in range(SPLIT, GROUPS):
+                second_product(second_banks[(a, n)], g, a, ROUND + n * BANK)
+            rotate_and_store(second_banks[(a, n)], a, ROUND + n * BANK)

@@ -20,8 +20,6 @@ TOKEN_TILES = 2
 LATENT = 8192
 GROUPS = LATENT // K_PASS
 Q_OUT = 2048
-ROUND = 1024
-ROUND_BANKS = ROUND // BANK
 HEAD = 128
 PLAIN = 64
 PAIRS = 32
@@ -29,7 +27,11 @@ HEADS_PER_BANK = BANK // HEAD
 POSITIONS = 64
 PLANES = 4
 LAG = 3
-SPLIT = 10
+
+FIRST_COL0 = 0
+MIDDLE_COL0 = BANK
+MIDDLE_BANKS = 2
+LAST_COL0 = 3 * BANK
 
 ROPE_BASE = 10000.0
 ROUND_MAGIC = 12582912.0
@@ -48,7 +50,7 @@ def tile_multilatentattention_pa_k_kernel(tc, x, Wqa_words, Wqa_scales, Wqb_word
         rows_pool = ctx.enter_context(tc.tile_pool(name="rows", bufs=4))
         grouped_pool = ctx.enter_context(tc.tile_pool(name="grouped", bufs=3))
         result_pool = ctx.enter_context(tc.tile_pool(name="result", bufs=4))
-        rope_pool = ctx.enter_context(tc.tile_pool(name="rope", bufs=2))
+        cross_pool = ctx.enter_context(tc.tile_pool(name="cross", bufs=2))
         psum = ctx.enter_context(tc.psum_pool(name="psum", bufs=1))
         ctx.enter_context(tc.manual_schedule())
 
@@ -135,39 +137,49 @@ def tile_multilatentattention_pa_k_kernel(tc, x, Wqa_words, Wqa_scales, Wqb_word
             cols = slice(first_group * K_PASS, (first_group + groups) * K_PASS)
             nc.sync.dma_start(out=wqa_words[:, cols].bitcast(I32), in_=wqa_dram[:, cols])
 
-        def load_wqb_words(g, q_round):
-            cols = slice(q_round * ROUND, (q_round + 1) * ROUND)
+        def load_wqb_words(g, col0, width):
+            cols = slice(col0, col0 + width)
             nc.sync.dma_start(
                 out=wqb_words[:, g, cols].bitcast(I32),
                 in_=Wqb_words[g].rearrange("p n t -> p (n t)").bitcast(I32)[:, cols],
             )
 
+        def in_range(groups):
+            return [g for g in groups if 0 <= g < GROUPS]
+
         nc.sync.dma_start(out=x_sb[:], in_=x_rows)
         load_wqa_planes()
-        for g in range(GROUPS + LAG):
-            if g < GROUPS and g % 2 == 0:
+        for g in range(0, GROUPS + LAG + 1, 2):
+            if g < GROUPS:
                 load_wqa_words(g, 2)
-            if g >= LAG:
-                if (g - LAG) % PLANES == 0:
-                    load_wqb_planes((g - LAG) // PLANES)
-                load_wqb_words(g - LAG, 0)
+            for old in in_range((g - LAG, g - LAG + 1)):
+                if old % PLANES == 0:
+                    load_wqb_planes(old // PLANES)
+                load_wqb_words(old, FIRST_COL0, BANK)
         for g in range(GROUPS):
-            load_wqb_words(g, 1)
-
-        x_words = x_sb[:].bitcast(F32)
-        x_flipped = psum.tile([P, TOKEN_TILES, 2, P], F32, tag="work2")
-        for a in range(TOKEN_TILES):
-            for u in range(2):
-                nc.tensor.transpose(out=x_flipped[:, a, u, :], in_=x_words[:, a, u : K_PASS // 2 : 2], identity=identity[:])
-        nc.vector.tensor_copy(out=x_grouped[:].bitcast(F32), in_=x_flipped[:].rearrange("p a u r -> p a r u"))
-        nc.vector.quantize_mx(
-            out=x_codes[:].bitcast(FP8X4),
-            scales=x_scales[:],
-            in_=x_grouped[:].rearrange("p a r t -> p (a r t)"),
-        )
+            load_wqb_words(g, MIDDLE_COL0, MIDDLE_BANKS * BANK)
+        for g in range(GROUPS):
+            load_wqb_words(g, LAST_COL0, BANK)
 
         def token_cols(a):
             return slice(a * P, (a + 1) * P)
+
+        x_words = x_sb[:].bitcast(F32)
+        for a in range(TOKEN_TILES):
+            x_flipped = psum.tile([P, 2, P], F32, tag="flip%d" % a, name="x_flipped")
+            for u in range(2):
+                nc.tensor.transpose(out=x_flipped[:, u, :], in_=x_words[:, a, u : K_PASS // 2 : 2], identity=identity[:])
+            side_by_side = x_flipped[:].rearrange("p u r -> p r u")
+            if a == 0:
+                nc.vector.tensor_copy(out=x_grouped[:, a, :, :].bitcast(F32), in_=side_by_side)
+            else:
+                nc.scalar.copy(out=x_grouped[:, a, :, :].bitcast(F32), in_=side_by_side)
+        for a in range(TOKEN_TILES):
+            nc.vector.quantize_mx(
+                out=x_codes[:, token_cols(a)].bitcast(FP8X4),
+                scales=x_scales[:, token_cols(a)],
+                in_=x_grouped[:, a, :, :].rearrange("p r t -> p (r t)"),
+            )
 
         cq_rows = {}
 
@@ -176,7 +188,7 @@ def tile_multilatentattention_pa_k_kernel(tc, x, Wqa_words, Wqa_scales, Wqb_word
             plane = g // PLANES
             block = g % PLANES
             for a in range(TOKEN_TILES):
-                bank = psum.tile([P, BANK], F32, tag="work%d" % a, name="cq_bank")
+                bank = psum.tile([P, BANK], F32, tag="cq%d" % (TOKEN_TILES * (g % 2) + a), name="cq_bank")
                 nc.tensor.matmul_mx(
                     out=bank[:],
                     lhsT=x_codes[:, token_cols(a)].bitcast(FP8X4),
@@ -194,7 +206,7 @@ def tile_multilatentattention_pa_k_kernel(tc, x, Wqa_words, Wqa_scales, Wqb_word
                     nc.vector.tensor_copy(out=sorted_view, in_=bank_view)
 
         def flip_and_quantise(g):
-            flipped = psum.tile([P, TOKEN_TILES, 2, P], F32, tag="work%d" % (2 + g % 2), name="flipped")
+            flipped = psum.tile([P, TOKEN_TILES, 2, P], F32, tag="flip%d" % (g % 2), name="flipped")
             for a in range(TOKEN_TILES):
                 for u in range(2):
                     nc.tensor.transpose(
@@ -219,71 +231,69 @@ def tile_multilatentattention_pa_k_kernel(tc, x, Wqa_words, Wqa_scales, Wqb_word
                 stop=(g == GROUPS - 1),
             )
 
-        sin_pairs = keep.tile([P, PAIRS, 2], F32)
         cos_pairs = keep.tile([P, PAIRS, 2], F32)
+        sin_planes = keep.tile([P, 2, PAIRS], F32)
 
         def rotate_and_store(bank, a, col0):
+            heads = bank[:].rearrange("r (h d) -> r h d", d=HEAD)
+            pairs = bank[:].rearrange("r (h j e) -> r h j e", h=HEADS_PER_BANK, e=2)
             result = result_pool.tile([P, HEADS_PER_BANK, HEAD], F32, name="result")
-            same = rope_pool.tile([P, HEADS_PER_BANK, 2 * PAIRS], F32, name="same")
-            cross = rope_pool.tile([P, HEADS_PER_BANK, 2 * PAIRS], F32, name="cross")
-            table_shape = [P, HEADS_PER_BANK, 2 * PAIRS]
-            nc.scalar.copy(out=result[:], in_=bank[:].rearrange("r (h d) -> r h d", d=HEAD))
+            cross = cross_pool.tile([P, 2, HEADS_PER_BANK, PAIRS], F32, name="cross")
             nc.vector.tensor_tensor(
-                out=same[:],
-                in0=result[:, :, PLAIN:HEAD],
-                in1=cos_pairs[:].rearrange("p j e -> p (j e)").unsqueeze(1).to_broadcast(table_shape),
-                op=ALU.mult,
-            )
-            nc.vector.tensor_tensor(
-                out=cross[:],
-                in0=result[:, :, PLAIN:HEAD],
-                in1=sin_pairs[:].rearrange("p j e -> p (j e)").unsqueeze(1).to_broadcast(table_shape),
+                out=result[:, :, PLAIN:HEAD],
+                in0=heads[:, :, PLAIN:HEAD],
+                in1=cos_pairs[:].rearrange("p j e -> p (j e)").unsqueeze(1).to_broadcast([P, HEADS_PER_BANK, 2 * PAIRS]),
                 op=ALU.mult,
             )
             for e in range(2):
                 nc.vector.tensor_tensor(
-                    out=result[:, :, PLAIN + e : HEAD : 2],
-                    in0=same[:, :, e : 2 * PAIRS : 2],
-                    in1=cross[:, :, 1 - e : 2 * PAIRS : 2],
-                    op=ALU.add,
+                    out=cross[:, e, :, :],
+                    in0=pairs[:, :, PAIRS : 2 * PAIRS, 1 - e],
+                    in1=sin_planes[:, e, :].unsqueeze(1).to_broadcast([P, HEADS_PER_BANK, PAIRS]),
+                    op=ALU.mult,
                 )
+            nc.scalar.copy(out=result[:, :, 0:PLAIN], in_=heads[:, :, 0:PLAIN])
+            rotated = result[:, :, PLAIN:HEAD].rearrange("r h (j e) -> r h j e", e=2)
+            nc.vector.tensor_tensor(
+                out=rotated, in0=rotated, in1=cross[:].rearrange("r e h j -> r h j e"), op=ALU.add
+            )
             nc.sync.dma_start(
                 out=out_rows[a * P : (a + 1) * P, col0 : col0 + BANK], in_=result[:].rearrange("r h d -> r (h d)")
             )
 
-        banks_of_round = [(a, n) for a in range(TOKEN_TILES) for n in range(ROUND_BANKS)]
-        first_banks = {}
-        for a, n in banks_of_round:
-            first_banks[(a, n)] = psum.tile([P, BANK], F32, tag="first%d" % (ROUND_BANKS * a + n), name="first_bank")
+        first_banks = [psum.tile([P, BANK], F32, tag="first%d" % a, name="first_bank") for a in range(TOKEN_TILES)]
+        for g in range(0, GROUPS + LAG + 1, 2):
+            for new in in_range((g, g + 1)):
+                first_product(new)
+            for old in in_range((g - LAG, g - LAG + 1)):
+                for a in range(TOKEN_TILES):
+                    second_product(first_banks[a], old, a, FIRST_COL0)
+            for new in in_range((g, g + 1)):
+                flip_and_quantise(new)
 
-        for g in range(GROUPS + LAG):
-            if g < GROUPS:
-                first_product(g)
-            if g >= LAG:
-                for a, n in banks_of_round:
-                    second_product(first_banks[(a, n)], g - LAG, a, n * BANK)
-            if g < GROUPS and g % 2 == 1:
-                flip_and_quantise(g - 1)
-                flip_and_quantise(g)
-
-        nc.scalar.activation(out=sin_pairs[:, :, 0], in_=frac[:, 0, :], func=FUNC.Sin, scale=2.0 * math.pi)
-        nc.scalar.activation(out=sin_pairs[:, :, 1], in_=frac[:, 0, :], func=FUNC.Sin, scale=-2.0 * math.pi)
+        nc.scalar.activation(out=sin_planes[:, 0, :], in_=frac[:, 0, :], func=FUNC.Sin, scale=-2.0 * math.pi)
+        nc.scalar.activation(out=sin_planes[:, 1, :], in_=frac[:, 0, :], func=FUNC.Sin, scale=2.0 * math.pi)
         nc.scalar.activation(
             out=cos_pairs[:],
             in_=frac[:, 1, :].unsqueeze(2).to_broadcast([P, PAIRS, 2]),
             func=FUNC.Sin,
             scale=2.0 * math.pi,
         )
-        for a, n in banks_of_round:
-            rotate_and_store(first_banks[(a, n)], a, n * BANK)
+        for a in range(TOKEN_TILES):
+            rotate_and_store(first_banks[a], a, FIRST_COL0)
 
-        second_banks = {}
-        for a, n in banks_of_round:
-            second_banks[(a, n)] = psum.tile([P, BANK], F32, tag="work%d" % (ROUND_BANKS * a + n), name="second_bank")
-        for g in range(SPLIT):
-            for a, n in banks_of_round:
-                second_product(second_banks[(a, n)], g, a, ROUND + n * BANK)
-        for a, n in banks_of_round:
-            for g in range(SPLIT, GROUPS):
-                second_product(second_banks[(a, n)], g, a, ROUND + n * BANK)
-            rotate_and_store(second_banks[(a, n)], a, ROUND + n * BANK)
+        middle = [(a, n) for a in range(TOKEN_TILES) for n in range(MIDDLE_BANKS)]
+        middle_banks = {}
+        for a, n in middle:
+            middle_banks[(a, n)] = psum.tile([P, BANK], F32, tag="cq%d" % (MIDDLE_BANKS * a + n), name="middle_bank")
+        for g in range(GROUPS):
+            for a, n in middle:
+                second_product(middle_banks[(a, n)], g, a, MIDDLE_COL0 + n * BANK)
+        for a, n in middle:
+            rotate_and_store(middle_banks[(a, n)], a, MIDDLE_COL0 + n * BANK)
+
+        for a in range(TOKEN_TILES):
+            last_bank = psum.tile([P, BANK], F32, tag="flip%d" % a, name="last_bank")
+            for g in range(GROUPS):
+                second_product(last_bank, g, a, LAST_COL0)
+            rotate_and_store(last_bank, a, LAST_COL0)

@@ -292,8 +292,9 @@ def tile_multilatentattention_pa_k_kernel(tc, x, Wqa_words, Wqa_scales, Wqb_word
         for a, n in middle:
             rotate_and_store(middle_banks[(a, n)], a, MIDDLE_COL0 + n * BANK)
 
+        last_banks = [psum.tile([P, BANK], F32, tag="flip%d" % a, name="last_bank") for a in range(TOKEN_TILES)]
+        for g in range(GROUPS):
+            for a in range(TOKEN_TILES):
+                second_product(last_banks[a], g, a, LAST_COL0)
         for a in range(TOKEN_TILES):
-            last_bank = psum.tile([P, BANK], F32, tag="flip%d" % a, name="last_bank")
-            for g in range(GROUPS):
-                second_product(last_bank, g, a, LAST_COL0)
-            rotate_and_store(last_bank, a, LAST_COL0)
+            rotate_and_store(last_banks[a], a, LAST_COL0)

@@ -26,6 +26,7 @@ PAIRS = 32
 HEADS_PER_BANK = BANK // HEAD
 POSITIONS = 64
 PLANES = 4
+SLOTS = 4
 LAG = 3
 
 FIRST_COL0 = 0
@@ -39,15 +40,19 @@ ROUND_MAGIC = 12582912.0
 FLOPS = 2 * 256 * 512 * LATENT + 2 * 256 * LATENT * Q_OUT
 
 
+def group_of(step):
+    return PLANES * (step % PLANES) + step // PLANES
+
+
 def tile_multilatentattention_pa_k_kernel(tc, x, Wqa_words, Wqa_scales, Wqb_words, Wqb_scales, out):
     nc = tc.nc
     x_rows = x.flatten_outer_dims().rearrange("(a r) d -> r a d", r=P)
     out_rows = out.rearrange("b s h d -> (b s) (h d)")
-    wqa_dram = Wqa_words[0].rearrange("p n t -> p (n t)").bitcast(I32)
+    wqa_dram = Wqa_words[0].rearrange("p n t -> p (n t)").bitcast(I32).rearrange("p (g n) -> p g n", g=GROUPS)
 
     with ExitStack() as ctx:
         keep = ctx.enter_context(tc.tile_pool(name="keep", bufs=1))
-        rows_pool = ctx.enter_context(tc.tile_pool(name="rows", bufs=4))
+        sorted_pool = ctx.enter_context(tc.tile_pool(name="sorted", bufs=3))
         grouped_pool = ctx.enter_context(tc.tile_pool(name="grouped", bufs=3))
         result_pool = ctx.enter_context(tc.tile_pool(name="result", bufs=4))
         cross_pool = ctx.enter_context(tc.tile_pool(name="cross", bufs=2))
@@ -59,9 +64,10 @@ def tile_multilatentattention_pa_k_kernel(tc, x, Wqa_words, Wqa_scales, Wqb_word
         x_grouped = keep.tile([P, TOKEN_TILES, P, 4], BF16, align_bytes=64)
         x_codes = keep.tile([P, TOKEN_TILES * P], U32, align_bytes=64)
         x_scales = keep.tile([P, TOKEN_TILES * P], U8, align_bytes=64)
-        wqa_words = keep.tile([P, LATENT], U32, align_bytes=64)
+        wqa_words = keep.tile([P, GROUPS, K_PASS], I32, align_bytes=64)
         wqa_planes = keep.tile([P, LATENT // PLANES], U8, align_bytes=64)
-        wqb_words = keep.tile([P, GROUPS, Q_OUT], U32, align_bytes=64)
+        wqa_sorted_planes = keep.tile([P, GROUPS // PLANES, K_PASS], U8, align_bytes=64)
+        wqb_words = keep.tile([P, GROUPS, Q_OUT], I32, align_bytes=64)
         wqb_planes = keep.tile([P, GROUPS // PLANES, Q_OUT], U8, align_bytes=64)
         cq_codes = keep.tile([P, GROUPS, TOKEN_TILES * P], U32, align_bytes=64)
         cq_scales = keep.tile([P, GROUPS, TOKEN_TILES * P], U8, align_bytes=64)
@@ -124,24 +130,27 @@ def tile_multilatentattention_pa_k_kernel(tc, x, Wqa_words, Wqa_scales, Wqb_word
                     .bitcast(I32),
                 )
 
-        def load_wqb_planes(plane_set):
+        def load_wqb_planes(block):
             for quadrant in range(4):
                 nc.sync.dma_start(
-                    out=wqb_planes[32 * quadrant : 32 * quadrant + 16, plane_set, :].bitcast(I32),
-                    in_=Wqb_scales[
-                        PLANES * plane_set : PLANES * (plane_set + 1), 4 * quadrant : 4 * quadrant + 4, :
+                    out=wqb_planes[32 * quadrant : 32 * quadrant + 16, block, :].bitcast(I32),
+                    in_=Wqb_scales.rearrange("(j s) r n -> s j r n", j=PLANES)[
+                        block, :, 4 * quadrant : 4 * quadrant + 4, :
                     ].bitcast(I32),
                 )
 
-        def load_wqa_words(first_group, groups):
-            cols = slice(first_group * K_PASS, (first_group + groups) * K_PASS)
-            nc.sync.dma_start(out=wqa_words[:, cols].bitcast(I32), in_=wqa_dram[:, cols])
+        def load_wqa_words(first_step, steps):
+            g = group_of(first_step)
+            nc.sync.dma_start(
+                out=wqa_words[:, first_step : first_step + steps, :],
+                in_=wqa_dram[:, g : g + PLANES * (steps - 1) + 1 : PLANES, :],
+            )
 
-        def load_wqb_words(g, col0, width):
+        def load_wqb_words(i, col0, width):
             cols = slice(col0, col0 + width)
             nc.sync.dma_start(
-                out=wqb_words[:, g, cols].bitcast(I32),
-                in_=Wqb_words[g].rearrange("p n t -> p (n t)").bitcast(I32)[:, cols],
+                out=wqb_words[:, i, cols],
+                in_=Wqb_words[group_of(i)].rearrange("p n t -> p (n t)").bitcast(I32)[:, cols],
             )
 
         def in_range(groups):
@@ -149,10 +158,10 @@ def tile_multilatentattention_pa_k_kernel(tc, x, Wqa_words, Wqa_scales, Wqb_word
 
         nc.sync.dma_start(out=x_sb[:], in_=x_rows)
         load_wqa_planes()
-        for g in range(0, GROUPS + LAG + 1, 2):
-            if g < GROUPS:
-                load_wqa_words(g, 2)
-            for old in in_range((g - LAG, g - LAG + 1)):
+        for i in range(0, GROUPS + LAG + 1, 2):
+            if i < GROUPS:
+                load_wqa_words(i, 2)
+            for old in in_range((i - LAG, i - LAG + 1)):
                 if old % PLANES == 0:
                     load_wqb_planes(old // PLANES)
                 load_wqb_words(old, FIRST_COL0, BANK)
@@ -164,6 +173,22 @@ def tile_multilatentattention_pa_k_kernel(tc, x, Wqa_words, Wqa_scales, Wqb_word
         def token_cols(a):
             return slice(a * P, (a + 1) * P)
 
+        sorted_words = {}
+        grouped = {}
+
+        def sort_planes(block):
+            nc.vector.tensor_copy(
+                out=wqa_sorted_planes[:, block, :].rearrange("p (t m) -> p m t", t=SLOTS),
+                in_=wqa_planes[:, block * K_PASS : (block + 1) * K_PASS].rearrange("p (m t) -> p m t", t=SLOTS),
+            )
+
+        def sort_words(i):
+            sorted_words[i] = sorted_pool.tile([P, K_PASS], I32, align_bytes=64, name="sorted_words")
+            nc.vector.tensor_copy(
+                out=sorted_words[i][:].rearrange("p (t m) -> p m t", t=SLOTS),
+                in_=wqa_words[:, i, :].rearrange("p (m t) -> p m t", t=SLOTS),
+            )
+
         x_words = x_sb[:].bitcast(F32)
         for a in range(TOKEN_TILES):
             x_flipped = psum.tile([P, 2, P], F32, tag="flip%d" % a, name="x_flipped")
@@ -174,6 +199,7 @@ def tile_multilatentattention_pa_k_kernel(tc, x, Wqa_words, Wqa_scales, Wqb_word
                 nc.vector.tensor_copy(out=x_grouped[:, a, :, :].bitcast(F32), in_=side_by_side)
             else:
                 nc.scalar.copy(out=x_grouped[:, a, :, :].bitcast(F32), in_=side_by_side)
+        sort_planes(0)
         for a in range(TOKEN_TILES):
             nc.vector.quantize_mx(
                 out=x_codes[:, token_cols(a)].bitcast(FP8X4),
@@ -181,43 +207,34 @@ def tile_multilatentattention_pa_k_kernel(tc, x, Wqa_words, Wqa_scales, Wqb_word
                 in_=x_grouped[:, a, :, :].rearrange("p r t -> p (r t)"),
             )
 
-        cq_rows = {}
-
-        def first_product(g):
-            cq_rows[g] = rows_pool.tile([P, TOKEN_TILES, 2, 2 * P], BF16, name="cq_rows")
-            plane = g // PLANES
-            block = g % PLANES
+        def first_product(i):
+            grouped[i] = grouped_pool.tile([P, TOKEN_TILES, P, SLOTS], BF16, align_bytes=64, name="grouped")
+            plane = i % PLANES
+            block = i // PLANES
             for a in range(TOKEN_TILES):
-                bank = psum.tile([P, BANK], F32, tag="cq%d" % (TOKEN_TILES * (g % 2) + a), name="cq_bank")
-                nc.tensor.matmul_mx(
-                    out=bank[:],
-                    lhsT=x_codes[:, token_cols(a)].bitcast(FP8X4),
-                    lhsT_scale=x_scales[:, token_cols(a)],
-                    rhs=wqa_words[:, g * K_PASS : (g + 1) * K_PASS].bitcast(FP8X4),
-                    rhs_scale=wqa_planes[4 * plane : P, block * K_PASS : (block + 1) * K_PASS],
-                    start=True,
-                    stop=True,
-                )
-                sorted_view = cq_rows[g][:, a, :, :].rearrange("r u (p e) -> r u p e", e=2)
-                bank_view = bank[:].rearrange("r (p u e) -> r u p e", u=2, e=2)
-                if a == 0:
-                    nc.scalar.copy(out=sorted_view, in_=bank_view)
-                else:
-                    nc.vector.tensor_copy(out=sorted_view, in_=bank_view)
-
-        def flip_and_quantise(g):
-            flipped = psum.tile([P, TOKEN_TILES, 2, P], F32, tag="flip%d" % (g % 2), name="flipped")
-            for a in range(TOKEN_TILES):
-                for u in range(2):
-                    nc.tensor.transpose(
-                        out=flipped[:, a, u, :], in_=cq_rows[g][:, a, u, :].bitcast(F32), identity=identity[:]
+                bank = psum.tile([P, SLOTS, P], F32, tag="cq%d" % (TOKEN_TILES * (i % 2) + a), name="cq_bank")
+                for t in range(SLOTS):
+                    features = slice(t * P, (t + 1) * P)
+                    nc.tensor.matmul_mx(
+                        out=bank[:, t, :],
+                        lhsT=sorted_words[i][:, features].bitcast(FP8X4),
+                        lhsT_scale=wqa_sorted_planes[4 * plane : P, block, features],
+                        rhs=x_codes[:, token_cols(a)].bitcast(FP8X4),
+                        rhs_scale=x_scales[:, token_cols(a)],
+                        start=True,
+                        stop=True,
                     )
-            grouped = grouped_pool.tile([P, TOKEN_TILES, P, 4], BF16, align_bytes=64, name="grouped")
-            nc.scalar.copy(out=grouped[:].bitcast(F32), in_=flipped[:].rearrange("p a u r -> p a r u"))
+                side_by_side = bank[:].rearrange("p t r -> p r t")
+                if a == 0:
+                    nc.scalar.copy(out=grouped[i][:, a, :, :], in_=side_by_side)
+                else:
+                    nc.vector.tensor_copy(out=grouped[i][:, a, :, :], in_=side_by_side)
+
+        def quantise(i):
             nc.vector.quantize_mx(
-                out=cq_codes[:, g, :].bitcast(FP8X4),
-                scales=cq_scales[:, g, :],
-                in_=grouped[:].rearrange("p a r t -> p (a r t)"),
+                out=cq_codes[:, i, :].bitcast(FP8X4),
+                scales=cq_scales[:, i, :],
+                in_=grouped[i][:].rearrange("p a r t -> p (a r t)"),
             )
 
         def second_product(bank, g, a, col0):
@@ -262,14 +279,20 @@ def tile_multilatentattention_pa_k_kernel(tc, x, Wqa_words, Wqa_scales, Wqb_word
             )
 
         first_banks = [psum.tile([P, BANK], F32, tag="first%d" % a, name="first_bank") for a in range(TOKEN_TILES)]
-        for g in range(0, GROUPS + LAG + 1, 2):
-            for new in in_range((g, g + 1)):
-                first_product(new)
-            for old in in_range((g - LAG, g - LAG + 1)):
+        sort_words(0)
+        sort_words(1)
+        for i in range(GROUPS + LAG):
+            if i < GROUPS:
+                first_product(i)
+            if i + 2 < GROUPS:
+                sort_words(i + 2)
+            if i + 1 < GROUPS // PLANES:
+                sort_planes(i + 1)
+            if 0 <= i - 1 < GROUPS:
+                quantise(i - 1)
+            if i >= LAG:
                 for a in range(TOKEN_TILES):
-                    second_product(first_banks[a], old, a, FIRST_COL0)
-            for new in in_range((g, g + 1)):
-                flip_and_quantise(new)
+                    second_product(first_banks[a], i - LAG, a, FIRST_COL0)
 
         nc.scalar.activation(out=sin_planes[:, 0, :], in_=frac[:, 0, :], func=FUNC.Sin, scale=-2.0 * math.pi)
         nc.scalar.activation(out=sin_planes[:, 1, :], in_=frac[:, 0, :], func=FUNC.Sin, scale=2.0 * math.pi)

@@ -29,10 +29,9 @@ PLANES = 4
 SLOTS = 4
 LAG = 3
 
-FIRST_COL0 = 0
-MIDDLE_COL0 = BANK
-MIDDLE_BANKS = 2
-LAST_COL0 = 3 * BANK
+ROUND = 2 * BANK
+ROUND_BANKS = 2
+SPLIT = 12
 
 ROPE_BASE = 10000.0
 ROUND_MAGIC = 12582912.0
@@ -54,7 +53,7 @@ def tile_multilatentattention_pa_k_kernel(tc, x, Wqa_words, Wqa_scales, Wqb_word
         keep = ctx.enter_context(tc.tile_pool(name="keep", bufs=1))
         sorted_pool = ctx.enter_context(tc.tile_pool(name="sorted", bufs=3))
         grouped_pool = ctx.enter_context(tc.tile_pool(name="grouped", bufs=3))
-        result_pool = ctx.enter_context(tc.tile_pool(name="result", bufs=4))
+        result_pool = ctx.enter_context(tc.tile_pool(name="result", bufs=8))
         cross_pool = ctx.enter_context(tc.tile_pool(name="cross", bufs=2))
         psum = ctx.enter_context(tc.psum_pool(name="psum", bufs=1))
         ctx.enter_context(tc.manual_schedule())
@@ -164,11 +163,12 @@ def tile_multilatentattention_pa_k_kernel(tc, x, Wqa_words, Wqa_scales, Wqb_word
             for old in in_range((i - LAG, i - LAG + 1)):
                 if old % PLANES == 0:
                     load_wqb_planes(old // PLANES)
-                load_wqb_words(old, FIRST_COL0, BANK)
-        for g in range(GROUPS):
-            load_wqb_words(g, MIDDLE_COL0, MIDDLE_BANKS * BANK)
-        for g in range(GROUPS):
-            load_wqb_words(g, LAST_COL0, BANK)
+                load_wqb_words(old, 0, ROUND)
+        for i in range(SPLIT):
+            load_wqb_words(i, ROUND, ROUND)
+        for n in range(ROUND_BANKS):
+            for i in range(SPLIT, GROUPS):
+                load_wqb_words(i, ROUND + n * BANK, BANK)
 
         def token_cols(a):
             return slice(a * P, (a + 1) * P)
@@ -191,7 +191,7 @@ def tile_multilatentattention_pa_k_kernel(tc, x, Wqa_words, Wqa_scales, Wqb_word
 
         x_words = x_sb[:].bitcast(F32)
         for a in range(TOKEN_TILES):
-            x_flipped = psum.tile([P, 2, P], F32, tag="flip%d" % a, name="x_flipped")
+            x_flipped = psum.tile([P, 2, P], F32, tag="cq%d" % a, name="x_flipped")
             for u in range(2):
                 nc.tensor.transpose(out=x_flipped[:, u, :], in_=x_words[:, a, u : K_PASS // 2 : 2], identity=identity[:])
             side_by_side = x_flipped[:].rearrange("p u r -> p r u")
@@ -278,7 +278,10 @@ def tile_multilatentattention_pa_k_kernel(tc, x, Wqa_words, Wqa_scales, Wqb_word
                 out=out_rows[a * P : (a + 1) * P, col0 : col0 + BANK], in_=result[:].rearrange("r h d -> r (h d)")
             )
 
-        first_banks = [psum.tile([P, BANK], F32, tag="first%d" % a, name="first_bank") for a in range(TOKEN_TILES)]
+        first = [(a, n) for n in range(ROUND_BANKS) for a in range(TOKEN_TILES)]
+        first_banks = {}
+        for a, n in first:
+            first_banks[(a, n)] = psum.tile([P, BANK], F32, tag="q%d%d" % (a, n), name="first_bank")
         sort_words(0)
         sort_words(1)
         for i in range(GROUPS + LAG):
@@ -291,8 +294,8 @@ def tile_multilatentattention_pa_k_kernel(tc, x, Wqa_words, Wqa_scales, Wqb_word
             if 0 <= i - 1 < GROUPS:
                 quantise(i - 1)
             if i >= LAG:
-                for a in range(TOKEN_TILES):
-                    second_product(first_banks[a], i - LAG, a, FIRST_COL0)
+                for a, n in first:
+                    second_product(first_banks[(a, n)], i - LAG, a, n * BANK)
 
         nc.scalar.activation(out=sin_planes[:, 0, :], in_=frac[:, 0, :], func=FUNC.Sin, scale=-2.0 * math.pi)
         nc.scalar.activation(out=sin_planes[:, 1, :], in_=frac[:, 0, :], func=FUNC.Sin, scale=2.0 * math.pi)
@@ -302,22 +305,18 @@ def tile_multilatentattention_pa_k_kernel(tc, x, Wqa_words, Wqa_scales, Wqb_word
             func=FUNC.Sin,
             scale=2.0 * math.pi,
         )
-        for a in range(TOKEN_TILES):
-            rotate_and_store(first_banks[a], a, FIRST_COL0)
+        for a, n in first:
+            rotate_and_store(first_banks[(a, n)], a, n * BANK)
 
-        middle = [(a, n) for a in range(TOKEN_TILES) for n in range(MIDDLE_BANKS)]
-        middle_banks = {}
-        for a, n in middle:
-            middle_banks[(a, n)] = psum.tile([P, BANK], F32, tag="cq%d" % (MIDDLE_BANKS * a + n), name="middle_bank")
-        for g in range(GROUPS):
-            for a, n in middle:
-                second_product(middle_banks[(a, n)], g, a, MIDDLE_COL0 + n * BANK)
-        for a, n in middle:
-            rotate_and_store(middle_banks[(a, n)], a, MIDDLE_COL0 + n * BANK)
-
-        last_banks = [psum.tile([P, BANK], F32, tag="flip%d" % a, name="last_bank") for a in range(TOKEN_TILES)]
-        for g in range(GROUPS):
+        last_banks = {}
+        for a, n in first:
+            last_banks[(a, n)] = psum.tile([P, BANK], F32, tag="cq%d" % (ROUND_BANKS * a + n), name="last_bank")
+        for i in range(SPLIT):
+            for a, n in first:
+                second_product(last_banks[(a, n)], i, a, ROUND + n * BANK)
+        for n in range(ROUND_BANKS):
+            for i in range(SPLIT, GROUPS):
+                for a in range(TOKEN_TILES):
+                    second_product(last_banks[(a, n)], i, a, ROUND + n * BANK)
             for a in range(TOKEN_TILES):
-                second_product(last_banks[a], g, a, LAST_COL0)
-        for a in range(TOKEN_TILES):
-            rotate_and_store(last_banks[a], a, LAST_COL0)
+                rotate_and_store(last_banks[(a, n)], a, ROUND + n * BANK)

@@ -81,6 +81,18 @@ def tile_multilatentattention_pa_k_kernel(tc, x, Wqa_words, Wqa_scales, Wqb_word
 
         make_identity(nc, identity[:])
 
+        def load_wqb_planes(block):
+            for quadrant in range(4):
+                nc.gpsimd.dma_start(
+                    out=wqb_planes[32 * quadrant : 32 * quadrant + 16, block, :].bitcast(F32),
+                    in_=Wqb_scales.rearrange("(j s) r n -> s j r n", j=PLANES)[
+                        block, :, 4 * quadrant : 4 * quadrant + 4, :
+                    ].bitcast(F32),
+                )
+
+        for block in range(2):
+            load_wqb_planes(block)
+
         inv_freq = keep.tile([P, PAIRS], F32)
         position = keep.tile([P, PAIRS], F32)
         angle = keep.tile([P, PAIRS], F32)
@@ -120,6 +132,9 @@ def tile_multilatentattention_pa_k_kernel(tc, x, Wqa_words, Wqa_scales, Wqb_word
         nc.gpsimd.tensor_single_scalar(out=whole[:], in_=lifted[:], scalar=ROUND_MAGIC, op=ALU.subtract)
         nc.gpsimd.tensor_tensor(out=frac[:], in0=turns[:], in1=whole[:], op=ALU.subtract)
 
+        for block in range(2, GROUPS // PLANES):
+            load_wqb_planes(block)
+
         def load_wqa_planes():
             for quadrant in range(4):
                 nc.sync.dma_start(
@@ -127,15 +142,6 @@ def tile_multilatentattention_pa_k_kernel(tc, x, Wqa_words, Wqa_scales, Wqb_word
                     in_=Wqa_scales[0, 4 * quadrant : 4 * quadrant + 4, :]
                     .rearrange("r (j n) -> j r n", j=PLANES)
                     .bitcast(I32),
-                )
-
-        def load_wqb_planes(block):
-            for quadrant in range(4):
-                nc.sync.dma_start(
-                    out=wqb_planes[32 * quadrant : 32 * quadrant + 16, block, :].bitcast(I32),
-                    in_=Wqb_scales.rearrange("(j s) r n -> s j r n", j=PLANES)[
-                        block, :, 4 * quadrant : 4 * quadrant + 4, :
-                    ].bitcast(I32),
                 )
 
         def load_wqa_words(first_step, steps):
@@ -161,8 +167,6 @@ def tile_multilatentattention_pa_k_kernel(tc, x, Wqa_words, Wqa_scales, Wqb_word
             if i < GROUPS:
                 load_wqa_words(i, 2)
             for old in in_range((i - LAG, i - LAG + 1)):
-                if old % PLANES == 0:
-                    load_wqb_planes(old // PLANES)
                 load_wqb_words(old, 0, ROUND)
         for i in range(SPLIT):
             load_wqb_words(i, ROUND, ROUND)

@@ -72,7 +72,8 @@ def tile_multilatentattention_pa_k_kernel(tc, x, Wqa_words, Wqa_scales, Wqb_word
         cq_scales = keep.tile([P, GROUPS, TOKEN_TILES * P], U8, align_bytes=64)
 
         nc.vector.memset(wqa_planes[:].bitcast(I32), 0)
-        nc.vector.memset(wqb_planes[:].bitcast(I32), 0)
+        for block in range(GROUPS // PLANES):
+            nc.vector.memset(wqb_planes[:, block, :].bitcast(I32), 0)
 
         zero = keep.tile([P, 1], F32)
         warm = keep.tile([P, 1], F32)
@@ -81,17 +82,17 @@ def tile_multilatentattention_pa_k_kernel(tc, x, Wqa_words, Wqa_scales, Wqb_word
 
         make_identity(nc, identity[:])
 
-        def load_wqb_planes(block):
+        def load_wqb_planes(queue, dtype, block):
             for quadrant in range(4):
-                nc.gpsimd.dma_start(
-                    out=wqb_planes[32 * quadrant : 32 * quadrant + 16, block, :].bitcast(F32),
+                queue.dma_start(
+                    out=wqb_planes[32 * quadrant : 32 * quadrant + 16, block, :].bitcast(dtype),
                     in_=Wqb_scales.rearrange("(j s) r n -> s j r n", j=PLANES)[
                         block, :, 4 * quadrant : 4 * quadrant + 4, :
-                    ].bitcast(F32),
+                    ].bitcast(dtype),
                 )
 
-        for block in range(2):
-            load_wqb_planes(block)
+        for block in range(1, GROUPS // PLANES):
+            load_wqb_planes(nc.gpsimd, F32, block)
 
         inv_freq = keep.tile([P, PAIRS], F32)
         position = keep.tile([P, PAIRS], F32)
@@ -132,9 +133,6 @@ def tile_multilatentattention_pa_k_kernel(tc, x, Wqa_words, Wqa_scales, Wqb_word
         nc.gpsimd.tensor_single_scalar(out=whole[:], in_=lifted[:], scalar=ROUND_MAGIC, op=ALU.subtract)
         nc.gpsimd.tensor_tensor(out=frac[:], in0=turns[:], in1=whole[:], op=ALU.subtract)
 
-        for block in range(2, GROUPS // PLANES):
-            load_wqb_planes(block)
-
         def load_wqa_planes():
             for quadrant in range(4):
                 nc.sync.dma_start(
@@ -167,6 +165,8 @@ def tile_multilatentattention_pa_k_kernel(tc, x, Wqa_words, Wqa_scales, Wqb_word
             if i < GROUPS:
                 load_wqa_words(i, 2)
             for old in in_range((i - LAG, i - LAG + 1)):
+                if old == 0:
+                    load_wqb_planes(nc.sync, I32, 0)
                 load_wqb_words(old, 0, ROUND)
         for i in range(SPLIT):
             load_wqb_words(i, ROUND, ROUND)

@@ -39,15 +39,11 @@ ROUND_MAGIC = 12582912.0
 FLOPS = 2 * 256 * 512 * LATENT + 2 * 256 * LATENT * Q_OUT
 
 
-def group_of(step):
-    return PLANES * (step % PLANES) + step // PLANES
-
-
 def tile_multilatentattention_pa_k_kernel(tc, x, Wqa_words, Wqa_scales, Wqb_words, Wqb_scales, out):
     nc = tc.nc
     x_rows = x.flatten_outer_dims().rearrange("(a r) d -> r a d", r=P)
     out_rows = out.rearrange("b s h d -> (b s) (h d)")
-    wqa_dram = Wqa_words[0].rearrange("p n t -> p (n t)").bitcast(I32).rearrange("p (g n) -> p g n", g=GROUPS)
+    wqa_dram = Wqa_words[0].rearrange("p n t -> p (n t)").bitcast(I32)
 
     with ExitStack() as ctx:
         keep = ctx.enter_context(tc.tile_pool(name="keep", bufs=1))
@@ -72,7 +68,7 @@ def tile_multilatentattention_pa_k_kernel(tc, x, Wqa_words, Wqa_scales, Wqb_word
         cq_scales = keep.tile([P, GROUPS, TOKEN_TILES * P], U8, align_bytes=64)
 
         nc.vector.memset(wqa_planes[:].bitcast(I32), 0)
-        for block in range(GROUPS // PLANES):
+        for block in (1, 0, 2, 3):
             nc.vector.memset(wqb_planes[:, block, :].bitcast(I32), 0)
 
         zero = keep.tile([P, 1], F32)
@@ -86,8 +82,8 @@ def tile_multilatentattention_pa_k_kernel(tc, x, Wqa_words, Wqa_scales, Wqb_word
             for quadrant in range(4):
                 queue.dma_start(
                     out=wqb_planes[32 * quadrant : 32 * quadrant + 16, block, :].bitcast(dtype),
-                    in_=Wqb_scales.rearrange("(j s) r n -> s j r n", j=PLANES)[
-                        block, :, 4 * quadrant : 4 * quadrant + 4, :
+                    in_=Wqb_scales[
+                        PLANES * block : PLANES * (block + 1), 4 * quadrant : 4 * quadrant + 4, :
                     ].bitcast(dtype),
                 )
 
@@ -142,37 +138,35 @@ def tile_multilatentattention_pa_k_kernel(tc, x, Wqa_words, Wqa_scales, Wqb_word
                     .bitcast(I32),
                 )
 
-        def load_wqa_words(first_step, steps):
-            g = group_of(first_step)
+        def load_wqa_words(g, groups):
             nc.sync.dma_start(
-                out=wqa_words[:, first_step : first_step + steps, :],
-                in_=wqa_dram[:, g : g + PLANES * (steps - 1) + 1 : PLANES, :],
+                out=wqa_words[:, g : g + groups, :].rearrange("p g n -> p (g n)"),
+                in_=wqa_dram[:, g * K_PASS : (g + groups) * K_PASS],
             )
 
-        def load_wqb_words(i, col0, width):
+        def load_wqb_words(g, groups, col0, width):
             cols = slice(col0, col0 + width)
             nc.sync.dma_start(
-                out=wqb_words[:, i, cols],
-                in_=Wqb_words[group_of(i)].rearrange("p n t -> p (n t)").bitcast(I32)[:, cols],
+                out=wqb_words[:, g : g + groups, cols],
+                in_=Wqb_words.rearrange("g p n t -> p g (n t)").bitcast(I32)[:, g : g + groups, cols],
             )
-
-        def in_range(groups):
-            return [g for g in groups if 0 <= g < GROUPS]
 
         nc.sync.dma_start(out=x_sb[:], in_=x_rows)
         load_wqa_planes()
-        for i in range(0, GROUPS + LAG + 1, 2):
-            if i < GROUPS:
-                load_wqa_words(i, 2)
-            for old in in_range((i - LAG, i - LAG + 1)):
-                if old == 0:
-                    load_wqb_planes(nc.sync, I32, 0)
-                load_wqb_words(old, 0, ROUND)
-        for i in range(SPLIT):
-            load_wqb_words(i, ROUND, ROUND)
+        for g in range(0, GROUPS, 2):
+            load_wqa_words(g, 2)
+            if g == 2:
+                load_wqb_planes(nc.sync, I32, 0)
+            for old in (g - 3, g - 2):
+                if old >= 0:
+                    load_wqb_words(old, 1, 0, ROUND)
+        for old in range(GROUPS - 3, GROUPS):
+            load_wqb_words(old, 1, 0, ROUND)
+        for g in range(SPLIT):
+            load_wqb_words(g, 1, ROUND, ROUND)
         for n in range(ROUND_BANKS):
-            for i in range(SPLIT, GROUPS):
-                load_wqb_words(i, ROUND + n * BANK, BANK)
+            for g in range(SPLIT, GROUPS, 2):
+                load_wqb_words(g, 2, ROUND + n * BANK, BANK)
 
         def token_cols(a):
             return slice(a * P, (a + 1) * P)
@@ -213,8 +207,8 @@ def tile_multilatentattention_pa_k_kernel(tc, x, Wqa_words, Wqa_scales, Wqb_word
 
         def first_product(i):
             grouped[i] = grouped_pool.tile([P, TOKEN_TILES, P, SLOTS], BF16, align_bytes=64, name="grouped")
-            plane = i % PLANES
-            block = i // PLANES
+            plane = i // PLANES
+            block = i % PLANES
             for a in range(TOKEN_TILES):
                 bank = psum.tile([P, SLOTS, P], F32, tag="cq%d" % (TOKEN_TILES * (i % 2) + a), name="cq_bank")
                 for t in range(SLOTS):

@@ -188,6 +188,7 @@ def tile_multilatentattention_pa_k_kernel(tc, x, Wqa_words, Wqa_scales, Wqb_word
             )
 
         x_words = x_sb[:].bitcast(F32)
+        sort_planes(0)
         for a in range(TOKEN_TILES):
             x_flipped = psum.tile([P, 2, P], F32, tag="cq%d" % a, name="x_flipped")
             for u in range(2):
@@ -197,7 +198,6 @@ def tile_multilatentattention_pa_k_kernel(tc, x, Wqa_words, Wqa_scales, Wqb_word
                 nc.vector.tensor_copy(out=x_grouped[:, a, :, :].bitcast(F32), in_=side_by_side)
             else:
                 nc.scalar.copy(out=x_grouped[:, a, :, :].bitcast(F32), in_=side_by_side)
-        sort_planes(0)
         for a in range(TOKEN_TILES):
             nc.vector.quantize_mx(
                 out=x_codes[:, token_cols(a)].bitcast(FP8X4),
@@ -281,16 +281,16 @@ def tile_multilatentattention_pa_k_kernel(tc, x, Wqa_words, Wqa_scales, Wqb_word
         for a, n in first:
             first_banks[(a, n)] = psum.tile([P, BANK], F32, tag="q%d%d" % (a, n), name="first_bank")
         sort_words(0)
+        for block in range(1, GROUPS // PLANES):
+            sort_planes(block)
         sort_words(1)
         for i in range(GROUPS + LAG):
             if i < GROUPS:
                 first_product(i)
-            if i + 2 < GROUPS:
-                sort_words(i + 2)
-            if i + 1 < GROUPS // PLANES:
-                sort_planes(i + 1)
             if 0 <= i - 1 < GROUPS:
                 quantise(i - 1)
+            if i + 2 < GROUPS:
+                sort_words(i + 2)
             if i >= LAG:
                 for a, n in first:
                     second_product(first_banks[(a, n)], i - LAG, a, n * BANK)
@@ -313,8 +313,9 @@ def tile_multilatentattention_pa_k_kernel(tc, x, Wqa_words, Wqa_scales, Wqb_word
             for a, n in first:
                 second_product(last_banks[(a, n)], i, a, ROUND + n * BANK)
         for n in range(ROUND_BANKS):
-            for i in range(SPLIT, GROUPS):
+            for i in range(SPLIT, GROUPS, 2):
                 for a in range(TOKEN_TILES):
                     second_product(last_banks[(a, n)], i, a, ROUND + n * BANK)
+                    second_product(last_banks[(a, n)], i + 1, a, ROUND + n * BANK)
             for a in range(TOKEN_TILES):
                 rotate_and_store(last_banks[(a, n)], a, ROUND + n * BANK)

@@ -23,15 +23,14 @@ Q_OUT = 2048
 HEAD = 128
 PLAIN = 64
 PAIRS = 32
-HEADS_PER_BANK = BANK // HEAD
 POSITIONS = 64
 PLANES = 4
 SLOTS = 4
-LAG = 3
+LAG = 2
 
 ROUND = 2 * BANK
 ROUND_BANKS = 2
-SPLIT = 12
+SPLIT = 8
 
 ROPE_BASE = 10000.0
 ROUND_MAGIC = 12582912.0
@@ -154,19 +153,25 @@ def tile_multilatentattention_pa_k_kernel(tc, x, Wqa_words, Wqa_scales, Wqb_word
         nc.sync.dma_start(out=x_sb[:], in_=x_rows)
         load_wqa_planes()
         for g in range(0, GROUPS, 2):
-            load_wqa_words(g, 2)
-            if g == 2:
+            if g == 0:
+                load_wqa_words(0, 1)
+                load_wqa_words(1, 1)
+            else:
+                load_wqa_words(g, 2)
+            if g == LAG:
                 load_wqb_planes(nc.sync, I32, 0)
-            for old in (g - 3, g - 2):
+            for old in (g - LAG, g - LAG + 1):
                 if old >= 0:
                     load_wqb_words(old, 1, 0, ROUND)
-        for old in range(GROUPS - 3, GROUPS):
+        for old in range(GROUPS - LAG, GROUPS):
             load_wqb_words(old, 1, 0, ROUND)
         for g in range(SPLIT):
             load_wqb_words(g, 1, ROUND, ROUND)
         for n in range(ROUND_BANKS):
-            for g in range(SPLIT, GROUPS, 2):
+            for g in range(SPLIT, GROUPS - 2, 2):
                 load_wqb_words(g, 2, ROUND + n * BANK, BANK)
+            for g in range(GROUPS - 2, GROUPS):
+                load_wqb_words(g, 1, ROUND + n * BANK, BANK)
 
         def token_cols(a):
             return slice(a * P, (a + 1) * P)
@@ -188,7 +193,6 @@ def tile_multilatentattention_pa_k_kernel(tc, x, Wqa_words, Wqa_scales, Wqb_word
             )
 
         x_words = x_sb[:].bitcast(F32)
-        sort_planes(0)
         for a in range(TOKEN_TILES):
             x_flipped = psum.tile([P, 2, P], F32, tag="cq%d" % a, name="x_flipped")
             for u in range(2):
@@ -198,6 +202,7 @@ def tile_multilatentattention_pa_k_kernel(tc, x, Wqa_words, Wqa_scales, Wqb_word
                 nc.vector.tensor_copy(out=x_grouped[:, a, :, :].bitcast(F32), in_=side_by_side)
             else:
                 nc.scalar.copy(out=x_grouped[:, a, :, :].bitcast(F32), in_=side_by_side)
+        sort_planes(0)
         for a in range(TOKEN_TILES):
             nc.vector.quantize_mx(
                 out=x_codes[:, token_cols(a)].bitcast(FP8X4),
@@ -223,7 +228,7 @@ def tile_multilatentattention_pa_k_kernel(tc, x, Wqa_words, Wqa_scales, Wqb_word
                         stop=True,
                     )
                 side_by_side = bank[:].rearrange("p t r -> p r t")
-                if a == 0:
+                if a == 0 or i % 2 == 1:
                     nc.scalar.copy(out=grouped[i][:, a, :, :], in_=side_by_side)
                 else:
                     nc.vector.tensor_copy(out=grouped[i][:, a, :, :], in_=side_by_side)
@@ -235,45 +240,44 @@ def tile_multilatentattention_pa_k_kernel(tc, x, Wqa_words, Wqa_scales, Wqb_word
                 in_=grouped[i][:].rearrange("p a r t -> p (a r t)"),
             )
 
-        def second_product(bank, g, a, col0):
+        def second_product(bank, g, a, col0, width=BANK):
             nc.tensor.matmul_mx(
-                out=bank[:],
+                out=bank,
                 lhsT=cq_codes[:, g, token_cols(a)].bitcast(FP8X4),
                 lhsT_scale=cq_scales[:, g, token_cols(a)],
-                rhs=wqb_words[:, g, col0 : col0 + BANK].bitcast(FP8X4),
-                rhs_scale=wqb_planes[4 * (g % PLANES) : P, g // PLANES, col0 : col0 + BANK],
+                rhs=wqb_words[:, g, col0 : col0 + width].bitcast(FP8X4),
+                rhs_scale=wqb_planes[4 * (g % PLANES) : P, g // PLANES, col0 : col0 + width],
                 start=(g == 0),
                 stop=(g == GROUPS - 1),
             )
 
         cos_pairs = keep.tile([P, PAIRS, 2], F32)
-        sin_planes = keep.tile([P, 2, PAIRS], F32)
+        sin_pairs = keep.tile([P, PAIRS, 2], F32)
 
-        def rotate_and_store(bank, a, col0):
-            heads = bank[:].rearrange("r (h d) -> r h d", d=HEAD)
-            pairs = bank[:].rearrange("r (h j e) -> r h j e", h=HEADS_PER_BANK, e=2)
-            result = result_pool.tile([P, HEADS_PER_BANK, HEAD], F32, name="result")
-            cross = cross_pool.tile([P, 2, HEADS_PER_BANK, PAIRS], F32, name="cross")
+        def rotate_and_store(bank, a, col0, width=BANK):
+            count = width // HEAD
+            heads = bank.rearrange("r (h d) -> r h d", d=HEAD)
+            pairs = bank.rearrange("r (h j e) -> r h j e", h=count, e=2)
+            result = result_pool.tile([P, count, HEAD], F32, name="result")
+            cross = cross_pool.tile([P, count, 2 * PAIRS], F32, name="cross")
             nc.vector.tensor_tensor(
                 out=result[:, :, PLAIN:HEAD],
                 in0=heads[:, :, PLAIN:HEAD],
-                in1=cos_pairs[:].rearrange("p j e -> p (j e)").unsqueeze(1).to_broadcast([P, HEADS_PER_BANK, 2 * PAIRS]),
+                in1=cos_pairs[:].rearrange("p j e -> p (j e)").unsqueeze(1).to_broadcast([P, count, 2 * PAIRS]),
                 op=ALU.mult,
             )
-            for e in range(2):
-                nc.vector.tensor_tensor(
-                    out=cross[:, e, :, :],
-                    in0=pairs[:, :, PAIRS : 2 * PAIRS, 1 - e],
-                    in1=sin_planes[:, e, :].unsqueeze(1).to_broadcast([P, HEADS_PER_BANK, PAIRS]),
-                    op=ALU.mult,
-                )
-            nc.scalar.copy(out=result[:, :, 0:PLAIN], in_=heads[:, :, 0:PLAIN])
-            rotated = result[:, :, PLAIN:HEAD].rearrange("r h (j e) -> r h j e", e=2)
             nc.vector.tensor_tensor(
-                out=rotated, in0=rotated, in1=cross[:].rearrange("r e h j -> r h j e"), op=ALU.add
+                out=cross[:].rearrange("r h (j e) -> r h j e", e=2),
+                in0=pairs[:, :, PAIRS : 2 * PAIRS, ::-1],
+                in1=sin_pairs[:].unsqueeze(1).to_broadcast([P, count, PAIRS, 2]),
+                op=ALU.mult,
+            )
+            nc.scalar.copy(out=result[:, :, 0:PLAIN], in_=heads[:, :, 0:PLAIN])
+            nc.vector.tensor_tensor(
+                out=result[:, :, PLAIN:HEAD], in0=result[:, :, PLAIN:HEAD], in1=cross[:], op=ALU.add
             )
             nc.sync.dma_start(
-                out=out_rows[a * P : (a + 1) * P, col0 : col0 + BANK], in_=result[:].rearrange("r h d -> r (h d)")
+                out=out_rows[a * P : (a + 1) * P, col0 : col0 + width], in_=result[:].rearrange("r h d -> r (h d)")
             )
 
         first = [(a, n) for n in range(ROUND_BANKS) for a in range(TOKEN_TILES)]
@@ -293,10 +297,10 @@ def tile_multilatentattention_pa_k_kernel(tc, x, Wqa_words, Wqa_scales, Wqb_word
                 sort_words(i + 2)
             if i >= LAG:
                 for a, n in first:
-                    second_product(first_banks[(a, n)], i - LAG, a, n * BANK)
+                    second_product(first_banks[(a, n)][:], i - LAG, a, n * BANK)
 
-        nc.scalar.activation(out=sin_planes[:, 0, :], in_=frac[:, 0, :], func=FUNC.Sin, scale=-2.0 * math.pi)
-        nc.scalar.activation(out=sin_planes[:, 1, :], in_=frac[:, 0, :], func=FUNC.Sin, scale=2.0 * math.pi)
+        nc.scalar.activation(out=sin_pairs[:, :, 0], in_=frac[:, 0, :], func=FUNC.Sin, scale=-2.0 * math.pi)
+        nc.scalar.activation(out=sin_pairs[:, :, 1], in_=frac[:, 0, :], func=FUNC.Sin, scale=2.0 * math.pi)
         nc.scalar.activation(
             out=cos_pairs[:],
             in_=frac[:, 1, :].unsqueeze(2).to_broadcast([P, PAIRS, 2]),
@@ -304,18 +308,17 @@ def tile_multilatentattention_pa_k_kernel(tc, x, Wqa_words, Wqa_scales, Wqb_word
             scale=2.0 * math.pi,
         )
         for a, n in first:
-            rotate_and_store(first_banks[(a, n)], a, n * BANK)
+            rotate_and_store(first_banks[(a, n)][:], a, n * BANK)
 
         last_banks = {}
         for a, n in first:
             last_banks[(a, n)] = psum.tile([P, BANK], F32, tag="cq%d" % (ROUND_BANKS * a + n), name="last_bank")
         for i in range(SPLIT):
             for a, n in first:
-                second_product(last_banks[(a, n)], i, a, ROUND + n * BANK)
+                second_product(last_banks[(a, n)][:], i, a, ROUND + n * BANK)
         for n in range(ROUND_BANKS):
-            for i in range(SPLIT, GROUPS, 2):
+            for i in range(SPLIT, GROUPS):
                 for a in range(TOKEN_TILES):
-                    second_product(last_banks[(a, n)], i, a, ROUND + n * BANK)
-                    second_product(last_banks[(a, n)], i + 1, a, ROUND + n * BANK)
+                    second_product(last_banks[(a, n)][:], i, a, ROUND + n * BANK)
             for a in range(TOKEN_TILES):
-                rotate_and_store(last_banks[(a, n)], a, ROUND + n * BANK)
+                rotate_and_store(last_banks[(a, n)][:], a, ROUND + n * BANK)

@@ -30,7 +30,8 @@ LAG = 2
 
 ROUND = 2 * BANK
 ROUND_BANKS = 2
-SPLIT = 8
+WIDE_FROM = 4
+SPLIT = 12
 
 ROPE_BASE = 10000.0
 ROUND_MAGIC = 12582912.0
@@ -49,7 +50,7 @@ def tile_multilatentattention_pa_k_kernel(tc, x, Wqa_words, Wqa_scales, Wqb_word
         sorted_pool = ctx.enter_context(tc.tile_pool(name="sorted", bufs=3))
         grouped_pool = ctx.enter_context(tc.tile_pool(name="grouped", bufs=3))
         result_pool = ctx.enter_context(tc.tile_pool(name="result", bufs=8))
-        cross_pool = ctx.enter_context(tc.tile_pool(name="cross", bufs=2))
+        cross_pool = ctx.enter_context(tc.tile_pool(name="cross", bufs=4))
         psum = ctx.enter_context(tc.psum_pool(name="psum", bufs=1))
         ctx.enter_context(tc.manual_schedule())
 
@@ -77,17 +78,18 @@ def tile_multilatentattention_pa_k_kernel(tc, x, Wqa_words, Wqa_scales, Wqb_word
 
         make_identity(nc, identity[:])
 
-        def load_wqb_planes(queue, dtype, block):
+        def load_wqb_planes(queue, dtype, block, cols=slice(0, Q_OUT)):
             for quadrant in range(4):
                 queue.dma_start(
-                    out=wqb_planes[32 * quadrant : 32 * quadrant + 16, block, :].bitcast(dtype),
+                    out=wqb_planes[32 * quadrant : 32 * quadrant + 16, block, cols].bitcast(dtype),
                     in_=Wqb_scales[
-                        PLANES * block : PLANES * (block + 1), 4 * quadrant : 4 * quadrant + 4, :
+                        PLANES * block : PLANES * (block + 1), 4 * quadrant : 4 * quadrant + 4, cols
                     ].bitcast(dtype),
                 )
 
         for block in range(1, GROUPS // PLANES):
             load_wqb_planes(nc.gpsimd, F32, block)
+        load_wqb_planes(nc.gpsimd, F32, 0, slice(ROUND, Q_OUT))
 
         inv_freq = keep.tile([P, PAIRS], F32)
         position = keep.tile([P, PAIRS], F32)
@@ -150,7 +152,8 @@ def tile_multilatentattention_pa_k_kernel(tc, x, Wqa_words, Wqa_scales, Wqb_word
                 in_=Wqb_words.rearrange("g p n t -> p g (n t)").bitcast(I32)[:, g : g + groups, cols],
             )
 
-        nc.sync.dma_start(out=x_sb[:], in_=x_rows)
+        for a in range(TOKEN_TILES):
+            nc.sync.dma_start(out=x_sb[:, a, :], in_=x_rows[:, a, :])
         load_wqa_planes()
         for g in range(0, GROUPS, 2):
             if g == 0:
@@ -159,7 +162,7 @@ def tile_multilatentattention_pa_k_kernel(tc, x, Wqa_words, Wqa_scales, Wqb_word
             else:
                 load_wqa_words(g, 2)
             if g == LAG:
-                load_wqb_planes(nc.sync, I32, 0)
+                load_wqb_planes(nc.sync, I32, 0, slice(0, ROUND))
             for old in (g - LAG, g - LAG + 1):
                 if old >= 0:
                     load_wqb_words(old, 1, 0, ROUND)
@@ -211,33 +214,41 @@ def tile_multilatentattention_pa_k_kernel(tc, x, Wqa_words, Wqa_scales, Wqb_word
             )
 
         def first_product(i):
-            grouped[i] = grouped_pool.tile([P, TOKEN_TILES, P, SLOTS], BF16, align_bytes=64, name="grouped")
+            grouped[i] = grouped_pool.tile([P, TOKEN_TILES * P, SLOTS], BF16, align_bytes=64, name="grouped")
             plane = i // PLANES
             block = i % PLANES
-            for a in range(TOKEN_TILES):
-                bank = psum.tile([P, SLOTS, P], F32, tag="cq%d" % (TOKEN_TILES * (i % 2) + a), name="cq_bank")
-                for t in range(SLOTS):
+            for half in range(2):
+                tag = "cq%d" % (2 * (i % 2) + half)
+                if i < WIDE_FROM:
+                    slots = range(SLOTS)
+                    tokens = token_cols(half)
+                    place = grouped[i][:, tokens, :]
+                else:
+                    slots = range(2 * half, 2 * half + 2)
+                    tokens = slice(0, TOKEN_TILES * P)
+                    place = grouped[i][:, :, 2 * half : 2 * half + 2]
+                bank = psum.tile([P, len(slots), BANK // len(slots)], F32, tag=tag, name="cq_bank")
+                for t in slots:
                     features = slice(t * P, (t + 1) * P)
                     nc.tensor.matmul_mx(
-                        out=bank[:, t, :],
+                        out=bank[:, t - slots[0], :],
                         lhsT=sorted_words[i][:, features].bitcast(FP8X4),
                         lhsT_scale=wqa_sorted_planes[4 * plane : P, block, features],
-                        rhs=x_codes[:, token_cols(a)].bitcast(FP8X4),
-                        rhs_scale=x_scales[:, token_cols(a)],
+                        rhs=x_codes[:, tokens].bitcast(FP8X4),
+                        rhs_scale=x_scales[:, tokens],
                         start=True,
                         stop=True,
                     )
-                side_by_side = bank[:].rearrange("p t r -> p r t")
-                if a == 0 or i % 2 == 1:
-                    nc.scalar.copy(out=grouped[i][:, a, :, :], in_=side_by_side)
+                if half == 0 or i % 2 == 1:
+                    nc.scalar.copy(out=place, in_=bank[:].rearrange("p t r -> p r t"))
                 else:
-                    nc.vector.tensor_copy(out=grouped[i][:, a, :, :], in_=side_by_side)
+                    nc.vector.tensor_copy(out=place, in_=bank[:].rearrange("p t r -> p r t"))
 
         def quantise(i):
             nc.vector.quantize_mx(
                 out=cq_codes[:, i, :].bitcast(FP8X4),
                 scales=cq_scales[:, i, :],
-                in_=grouped[i][:].rearrange("p a r t -> p (a r t)"),
+                in_=grouped[i][:].rearrange("p r t -> p (r t)"),
             )
 
         def second_product(bank, g, a, col0, width=BANK):
@@ -254,8 +265,8 @@ def tile_multilatentattention_pa_k_kernel(tc, x, Wqa_words, Wqa_scales, Wqb_word
         cos_pairs = keep.tile([P, PAIRS, 2], F32)
         sin_pairs = keep.tile([P, PAIRS, 2], F32)
 
-        def rotate_and_store(bank, a, col0, width=BANK):
-            count = width // HEAD
+        def rotate_and_store(bank, a, col0, last=False):
+            count = BANK // HEAD
             heads = bank.rearrange("r (h d) -> r h d", d=HEAD)
             pairs = bank.rearrange("r (h j e) -> r h j e", h=count, e=2)
             result = result_pool.tile([P, count, HEAD], F32, name="result")
@@ -273,11 +284,12 @@ def tile_multilatentattention_pa_k_kernel(tc, x, Wqa_words, Wqa_scales, Wqb_word
                 op=ALU.mult,
             )
             nc.scalar.copy(out=result[:, :, 0:PLAIN], in_=heads[:, :, 0:PLAIN])
-            nc.vector.tensor_tensor(
+            adder = nc.vector if last else nc.gpsimd
+            adder.tensor_tensor(
                 out=result[:, :, PLAIN:HEAD], in0=result[:, :, PLAIN:HEAD], in1=cross[:], op=ALU.add
             )
             nc.sync.dma_start(
-                out=out_rows[a * P : (a + 1) * P, col0 : col0 + width], in_=result[:].rearrange("r h d -> r (h d)")
+                out=out_rows[a * P : (a + 1) * P, col0 : col0 + BANK], in_=result[:].rearrange("r h d -> r (h d)")
             )
 
         first = [(a, n) for n in range(ROUND_BANKS) for a in range(TOKEN_TILES)]
@@ -321,4 +333,5 @@ def tile_multilatentattention_pa_k_kernel(tc, x, Wqa_words, Wqa_scales, Wqb_word
                 for a in range(TOKEN_TILES):
                     second_product(last_banks[(a, n)][:], i, a, ROUND + n * BANK)
             for a in range(TOKEN_TILES):
-                rotate_and_store(last_banks[(a, n)][:], a, ROUND + n * BANK)
+                is_last = (a, n) == (TOKEN_TILES - 1, ROUND_BANKS - 1)
+                rotate_and_store(last_banks[(a, n)][:], a, ROUND + n * BANK, last=is_last)

@@ -26,7 +26,7 @@ PAIRS = 32
 POSITIONS = 64
 PLANES = 4
 SLOTS = 4
-LAG = 2
+LAG = 3
 
 ROUND = 2 * BANK
 ROUND_BANKS = 2
@@ -161,7 +161,7 @@ def tile_multilatentattention_pa_k_kernel(tc, x, Wqa_words, Wqa_scales, Wqb_word
                 load_wqa_words(1, 1)
             else:
                 load_wqa_words(g, 2)
-            if g == LAG:
+            if g == 2:
                 load_wqb_planes(nc.sync, I32, 0, slice(0, ROUND))
             for old in (g - LAG, g - LAG + 1):
                 if old >= 0:
@@ -297,14 +297,15 @@ def tile_multilatentattention_pa_k_kernel(tc, x, Wqa_words, Wqa_scales, Wqb_word
         for a, n in first:
             first_banks[(a, n)] = psum.tile([P, BANK], F32, tag="q%d%d" % (a, n), name="first_bank")
         sort_words(0)
-        for block in range(1, GROUPS // PLANES):
-            sort_planes(block)
+        sort_planes(1)
         sort_words(1)
         for i in range(GROUPS + LAG):
             if i < GROUPS:
                 first_product(i)
             if 0 <= i - 1 < GROUPS:
                 quantise(i - 1)
+            if i + 2 < GROUPS // PLANES:
+                sort_planes(i + 2)
             if i + 2 < GROUPS:
                 sort_words(i + 2)
             if i >= LAG:
@@ -329,8 +330,11 @@ def tile_multilatentattention_pa_k_kernel(tc, x, Wqa_words, Wqa_scales, Wqb_word
             for a, n in first:
                 second_product(last_banks[(a, n)][:], i, a, ROUND + n * BANK)
         for n in range(ROUND_BANKS):
-            for i in range(SPLIT, GROUPS):
+            for i in range(SPLIT, GROUPS - 2):
                 for a in range(TOKEN_TILES):
+                    second_product(last_banks[(a, n)][:], i, a, ROUND + n * BANK)
+            for a in range(TOKEN_TILES):
+                for i in range(GROUPS - 2, GROUPS):
                     second_product(last_banks[(a, n)][:], i, a, ROUND + n * BANK)
             for a in range(TOKEN_TILES):
                 is_last = (a, n) == (TOKEN_TILES - 1, ROUND_BANKS - 1)

import math
from contextlib import ExitStack

import concourse.mybir as mybir
from concourse.masks import make_identity

F32 = mybir.dt.float32
BF16 = mybir.dt.bfloat16
I32 = mybir.dt.int32
U32 = mybir.dt.uint32
U8 = mybir.dt.uint8
FP8X4 = mybir.dt.float8_e4m3fn_x4
ALU = mybir.AluOpType
FUNC = mybir.ActivationFunctionType

P = 128
K_PASS = 512
BANK = 512
TOKEN_TILES = 2
LATENT = 8192
GROUPS = LATENT // K_PASS
Q_OUT = 2048
HEAD = 128
PLAIN = 64
PAIRS = 32
POSITIONS = 64
PLANES = 4
SLOTS = 4
LAG = 3

ROUND = 2 * BANK
ROUND_BANKS = 2
WIDE_FROM = 4
SPLIT = 12

ROPE_BASE = 10000.0
ROUND_MAGIC = 12582912.0

FLOPS = 2 * 256 * 512 * LATENT + 2 * 256 * LATENT * Q_OUT


def tile_multilatentattention_pa_k_kernel(tc, x, Wqa_words, Wqa_scales, Wqb_words, Wqb_scales, out):
    nc = tc.nc
    x_rows = x.flatten_outer_dims().rearrange("(a r) d -> r a d", r=P)
    out_rows = out.rearrange("b s h d -> (b s) (h d)")
    wqa_dram = Wqa_words[0].rearrange("p n t -> p (n t)").bitcast(I32)

    with ExitStack() as ctx:
        keep = ctx.enter_context(tc.tile_pool(name="keep", bufs=1))
        sorted_pool = ctx.enter_context(tc.tile_pool(name="sorted", bufs=3))
        grouped_pool = ctx.enter_context(tc.tile_pool(name="grouped", bufs=3))
        result_pool = ctx.enter_context(tc.tile_pool(name="result", bufs=8))
        cross_pool = ctx.enter_context(tc.tile_pool(name="cross", bufs=4))
        psum = ctx.enter_context(tc.psum_pool(name="psum", bufs=1))
        ctx.enter_context(tc.manual_schedule())

        x_sb = keep.tile([P, TOKEN_TILES, K_PASS], BF16)
        identity = keep.tile([P, P], F32)
        x_grouped = keep.tile([P, TOKEN_TILES, P, 4], BF16, align_bytes=64)
        x_codes = keep.tile([P, TOKEN_TILES * P], U32, align_bytes=64)
        x_scales = keep.tile([P, TOKEN_TILES * P], U8, align_bytes=64)
        wqa_words = keep.tile([P, GROUPS, K_PASS], I32, align_bytes=64)
        wqa_planes = keep.tile([P, LATENT // PLANES], U8, align_bytes=64)
        wqa_sorted_planes = keep.tile([P, GROUPS // PLANES, K_PASS], U8, align_bytes=64)
        wqb_words = keep.tile([P, GROUPS, Q_OUT], I32, align_bytes=64)
        wqb_planes = keep.tile([P, GROUPS // PLANES, Q_OUT], U8, align_bytes=64)
        cq_codes = keep.tile([P, GROUPS, TOKEN_TILES * P], U32, align_bytes=64)
        cq_scales = keep.tile([P, GROUPS, TOKEN_TILES * P], U8, align_bytes=64)

        nc.vector.memset(wqa_planes[:].bitcast(I32), 0)
        for block in (1, 0, 2, 3):
            nc.vector.memset(wqb_planes[:, block, :].bitcast(I32), 0)

        zero = keep.tile([P, 1], F32)
        warm = keep.tile([P, 1], F32)
        nc.vector.memset(zero[:], 0.0)
        nc.scalar.activation(out=warm[:], in_=zero[:], func=FUNC.Sin)

        make_identity(nc, identity[:])

        def load_wqb_planes(queue, dtype, block, cols=slice(0, Q_OUT)):
            for quadrant in range(4):
                queue.dma_start(
                    out=wqb_planes[32 * quadrant : 32 * quadrant + 16, block, cols].bitcast(dtype),
                    in_=Wqb_scales[
                        PLANES * block : PLANES * (block + 1), 4 * quadrant : 4 * quadrant + 4, cols
                    ].bitcast(dtype),
                )

        for block in range(1, GROUPS // PLANES):
            load_wqb_planes(nc.gpsimd, F32, block)
        load_wqb_planes(nc.gpsimd, F32, 0, slice(ROUND, Q_OUT))

        inv_freq = keep.tile([P, PAIRS], F32)
        position = keep.tile([P, PAIRS], F32)
        angle = keep.tile([P, PAIRS], F32)
        turns = keep.tile([P, 2, PAIRS], F32)
        lifted = keep.tile([P, 2, PAIRS], F32)
        whole = keep.tile([P, 2, PAIRS], F32)
        frac = keep.tile([P, 2, PAIRS], F32)
        nc.gpsimd.memset(inv_freq[:, 0:1], 1.0)
        for width in (1, 2, 4, 8, 16):
            nc.gpsimd.tensor_scalar(
                out=inv_freq[:, width : 2 * width],
                in0=inv_freq[:, 0:width],
                scalar1=ROPE_BASE ** (-2.0 * width / (2 * PAIRS)),
                scalar2=0.0,
                op0=ALU.mult,
                op1=ALU.add,
            )
        for half in range(P // POSITIONS):
            nc.gpsimd.iota(
                position[half * POSITIONS : (half + 1) * POSITIONS, :],
                pattern=[[0, PAIRS]],
                base=0,
                channel_multiplier=1,
                allow_small_or_imprecise_dtypes=True,
            )
        nc.gpsimd.tensor_tensor(out=angle[:], in0=position[:], in1=inv_freq[:], op=ALU.mult)
        for shifted in range(2):
            nc.gpsimd.tensor_scalar(
                out=turns[:, shifted, :],
                in0=angle[:],
                scalar1=1.0 / (2.0 * math.pi),
                scalar2=0.25 * shifted,
                op0=ALU.mult,
                op1=ALU.add,
            )
        nc.gpsimd.tensor_single_scalar(out=lifted[:], in_=turns[:], scalar=ROUND_MAGIC, op=ALU.add)
        nc.gpsimd.tensor_single_scalar(out=whole[:], in_=lifted[:], scalar=ROUND_MAGIC, op=ALU.subtract)
        nc.gpsimd.tensor_tensor(out=frac[:], in0=turns[:], in1=whole[:], op=ALU.subtract)

        def load_wqa_planes():
            for quadrant in range(4):
                nc.sync.dma_start(
                    out=wqa_planes[32 * quadrant : 32 * quadrant + 16, :].bitcast(I32),
                    in_=Wqa_scales[0, 4 * quadrant : 4 * quadrant + 4, :]
                    .rearrange("r (j n) -> j r n", j=PLANES)
                    .bitcast(I32),
                )

        def load_wqa_words(g, groups):
            nc.sync.dma_start(
                out=wqa_words[:, g : g + groups, :].rearrange("p g n -> p (g n)"),
                in_=wqa_dram[:, g * K_PASS : (g + groups) * K_PASS],
            )

        def load_wqb_words(g, groups, col0, width):
            cols = slice(col0, col0 + width)
            nc.sync.dma_start(
                out=wqb_words[:, g : g + groups, cols],
                in_=Wqb_words.rearrange("g p n t -> p g (n t)").bitcast(I32)[:, g : g + groups, cols],
            )

        for a in range(TOKEN_TILES):
            nc.sync.dma_start(out=x_sb[:, a, :], in_=x_rows[:, a, :])
        load_wqa_planes()
        for g in range(0, GROUPS, 2):
            if g == 0:
                load_wqa_words(0, 1)
                load_wqa_words(1, 1)
            else:
                load_wqa_words(g, 2)
            if g == 2:
                load_wqb_planes(nc.sync, I32, 0, slice(0, ROUND))
            for old in (g - LAG, g - LAG + 1):
                if old >= 0:
                    load_wqb_words(old, 1, 0, ROUND)
        for old in range(GROUPS - LAG, GROUPS):
            load_wqb_words(old, 1, 0, ROUND)
        for g in range(SPLIT):
            load_wqb_words(g, 1, ROUND, ROUND)
        for n in range(ROUND_BANKS):
            for g in range(SPLIT, GROUPS - 2, 2):
                load_wqb_words(g, 2, ROUND + n * BANK, BANK)
            for g in range(GROUPS - 2, GROUPS):
                load_wqb_words(g, 1, ROUND + n * BANK, BANK)

        def token_cols(a):
            return slice(a * P, (a + 1) * P)

        sorted_words = {}
        grouped = {}

        def sort_planes(block):
            nc.vector.tensor_copy(
                out=wqa_sorted_planes[:, block, :].rearrange("p (t m) -> p m t", t=SLOTS),
                in_=wqa_planes[:, block * K_PASS : (block + 1) * K_PASS].rearrange("p (m t) -> p m t", t=SLOTS),
            )

        def sort_words(i):
            sorted_words[i] = sorted_pool.tile([P, K_PASS], I32, align_bytes=64, name="sorted_words")
            nc.vector.tensor_copy(
                out=sorted_words[i][:].rearrange("p (t m) -> p m t", t=SLOTS),
                in_=wqa_words[:, i, :].rearrange("p (m t) -> p m t", t=SLOTS),
            )

        x_words = x_sb[:].bitcast(F32)
        for a in range(TOKEN_TILES):
            x_flipped = psum.tile([P, 2, P], F32, tag="cq%d" % a, name="x_flipped")
            for u in range(2):
                nc.tensor.transpose(out=x_flipped[:, u, :], in_=x_words[:, a, u : K_PASS // 2 : 2], identity=identity[:])
            side_by_side = x_flipped[:].rearrange("p u r -> p r u")
            if a == 0:
                nc.vector.tensor_copy(out=x_grouped[:, a, :, :].bitcast(F32), in_=side_by_side)
            else:
                nc.scalar.copy(out=x_grouped[:, a, :, :].bitcast(F32), in_=side_by_side)
        sort_planes(0)
        for a in range(TOKEN_TILES):
            nc.vector.quantize_mx(
                out=x_codes[:, token_cols(a)].bitcast(FP8X4),
                scales=x_scales[:, token_cols(a)],
                in_=x_grouped[:, a, :, :].rearrange("p r t -> p (r t)"),
            )

        def first_product(i):
            grouped[i] = grouped_pool.tile([P, TOKEN_TILES * P, SLOTS], BF16, align_bytes=64, name="grouped")
            plane = i // PLANES
            block = i % PLANES
            for half in range(2):
                tag = "cq%d" % (2 * (i % 2) + half)
                if i < WIDE_FROM:
                    slots = range(SLOTS)
                    tokens = token_cols(half)
                    place = grouped[i][:, tokens, :]
                else:
                    slots = range(2 * half, 2 * half + 2)
                    tokens = slice(0, TOKEN_TILES * P)
                    place = grouped[i][:, :, 2 * half : 2 * half + 2]
                bank = psum.tile([P, len(slots), BANK // len(slots)], F32, tag=tag, name="cq_bank")
                for t in slots:
                    features = slice(t * P, (t + 1) * P)
                    nc.tensor.matmul_mx(
                        out=bank[:, t - slots[0], :],
                        lhsT=sorted_words[i][:, features].bitcast(FP8X4),
                        lhsT_scale=wqa_sorted_planes[4 * plane : P, block, features],
                        rhs=x_codes[:, tokens].bitcast(FP8X4),
                        rhs_scale=x_scales[:, tokens],
                        start=True,
                        stop=True,
                    )
                if half == 0 or i % 2 == 1:
                    nc.scalar.copy(out=place, in_=bank[:].rearrange("p t r -> p r t"))
                else:
                    nc.vector.tensor_copy(out=place, in_=bank[:].rearrange("p t r -> p r t"))

        def quantise(i):
            nc.vector.quantize_mx(
                out=cq_codes[:, i, :].bitcast(FP8X4),
                scales=cq_scales[:, i, :],
                in_=grouped[i][:].rearrange("p r t -> p (r t)"),
            )

        def second_product(bank, g, a, col0, width=BANK):
            nc.tensor.matmul_mx(
                out=bank,
                lhsT=cq_codes[:, g, token_cols(a)].bitcast(FP8X4),
                lhsT_scale=cq_scales[:, g, token_cols(a)],
                rhs=wqb_words[:, g, col0 : col0 + width].bitcast(FP8X4),
                rhs_scale=wqb_planes[4 * (g % PLANES) : P, g // PLANES, col0 : col0 + width],
                start=(g == 0),
                stop=(g == GROUPS - 1),
            )

        cos_pairs = keep.tile([P, PAIRS, 2], F32)
        sin_pairs = keep.tile([P, PAIRS, 2], F32)

        def rotate_and_store(bank, a, col0, last=False):
            count = BANK // HEAD
            heads = bank.rearrange("r (h d) -> r h d", d=HEAD)
            pairs = bank.rearrange("r (h j e) -> r h j e", h=count, e=2)
            result = result_pool.tile([P, count, HEAD], F32, name="result")
            cross = cross_pool.tile([P, count, 2 * PAIRS], F32, name="cross")
            nc.vector.tensor_tensor(
                out=result[:, :, PLAIN:HEAD],
                in0=heads[:, :, PLAIN:HEAD],
                in1=cos_pairs[:].rearrange("p j e -> p (j e)").unsqueeze(1).to_broadcast([P, count, 2 * PAIRS]),
                op=ALU.mult,
            )
            nc.vector.tensor_tensor(
                out=cross[:].rearrange("r h (j e) -> r h j e", e=2),
                in0=pairs[:, :, PAIRS : 2 * PAIRS, ::-1],
                in1=sin_pairs[:].unsqueeze(1).to_broadcast([P, count, PAIRS, 2]),
                op=ALU.mult,
            )
            nc.scalar.copy(out=result[:, :, 0:PLAIN], in_=heads[:, :, 0:PLAIN])
            adder = nc.vector if last else nc.gpsimd
            adder.tensor_tensor(
                out=result[:, :, PLAIN:HEAD], in0=result[:, :, PLAIN:HEAD], in1=cross[:], op=ALU.add
            )
            nc.sync.dma_start(
                out=out_rows[a * P : (a + 1) * P, col0 : col0 + BANK], in_=result[:].rearrange("r h d -> r (h d)")
            )

        first = [(a, n) for n in range(ROUND_BANKS) for a in range(TOKEN_TILES)]
        first_banks = {}
        for a, n in first:
            first_banks[(a, n)] = psum.tile([P, BANK], F32, tag="q%d%d" % (a, n), name="first_bank")
        sort_words(0)
        sort_planes(1)
        sort_words(1)
        for i in range(GROUPS + LAG):
            if i < GROUPS:
                first_product(i)
            if 0 <= i - 1 < GROUPS:
                quantise(i - 1)
            if i + 2 < GROUPS // PLANES:
                sort_planes(i + 2)
            if i + 2 < GROUPS:
                sort_words(i + 2)
            if i >= LAG:
                for a, n in first:
                    second_product(first_banks[(a, n)][:], i - LAG, a, n * BANK)

        nc.scalar.activation(out=sin_pairs[:, :, 0], in_=frac[:, 0, :], func=FUNC.Sin, scale=-2.0 * math.pi)
        nc.scalar.activation(out=sin_pairs[:, :, 1], in_=frac[:, 0, :], func=FUNC.Sin, scale=2.0 * math.pi)
        nc.scalar.activation(
            out=cos_pairs[:],
            in_=frac[:, 1, :].unsqueeze(2).to_broadcast([P, PAIRS, 2]),
            func=FUNC.Sin,
            scale=2.0 * math.pi,
        )
        for a, n in first:
            rotate_and_store(first_banks[(a, n)][:], a, n * BANK)

        last_banks = {}
        for a, n in first:
            last_banks[(a, n)] = psum.tile([P, BANK], F32, tag="cq%d" % (ROUND_BANKS * a + n), name="last_bank")
        for i in range(SPLIT):
            for a, n in first:
                second_product(last_banks[(a, n)][:], i, a, ROUND + n * BANK)
        for n in range(ROUND_BANKS):
            for i in range(SPLIT, GROUPS - 2):
                for a in range(TOKEN_TILES):
                    second_product(last_banks[(a, n)][:], i, a, ROUND + n * BANK)
            for a in range(TOKEN_TILES):
                for i in range(GROUPS - 2, GROUPS):
                    second_product(last_banks[(a, n)][:], i, a, ROUND + n * BANK)
            for a in range(TOKEN_TILES):
                is_last = (a, n) == (TOKEN_TILES - 1, ROUND_BANKS - 1)
                rotate_and_store(last_banks[(a, n)][:], a, ROUND + n * BANK, last=is_last)
